import numpy as np
import ml_dtypes


def mxq(x, axis, fmt="e4m3"):
    dtype, down = {"e4m3": (ml_dtypes.float8_e4m3fn, 7), "e5m2": (ml_dtypes.float8_e5m2, 14)}[fmt]
    v = np.moveaxis(np.asarray(x, np.float32).astype(ml_dtypes.bfloat16).astype(np.float64), axis, -1)
    blocks = v.reshape(v.shape[:-1] + (-1, 32))
    amax = np.abs(blocks).max(-1, keepdims=True)
    byte = np.maximum(np.where(amax > 0, np.frexp(amax)[1] - 1 + 127, 0) - down, 1)
    scale = np.exp2(byte - 127.0)
    codes = (blocks / scale).astype(np.float32).astype(dtype).astype(np.float64)
    return np.moveaxis((codes * scale).reshape(v.shape), -1, axis)


WIDE = False


def mx_kscale(k):
    if not WIDE:
        return np.ones(k)
    levels = np.array([10, -10, 5, -5, 0])
    if k % 512:
        return np.exp2(np.random.permutation(np.resize(levels, k // 32))).repeat(32)
    a = np.empty((k // 512, 16))
    for p in range(k // 512):
        a[p, :8] = np.random.permutation(np.resize(levels, 8))
        for g in range(8):
            far = levels[np.abs(levels - a[p, g]) >= 10]
            a[p, g + 8] = far[np.random.randint(len(far))]
    return np.exp2(a.ravel()).repeat(32)


BF16 = ml_dtypes.bfloat16


def bf(x):
    return np.asarray(x, np.float32).astype(BF16)


def f64(x):
    return np.asarray(x).astype(np.float64)


N, N_CH, D, H = 1024, 2, 2, 512


def sigmoid(v):
    return 1.0 / (1.0 + np.exp(-v))


def setup_inputs():
    s = mx_kscale(N)
    u = mx_kscale(H)
    nh0 = bf(np.random.standard_normal((N, N_CH, H)))
    neighbour_c = bf(np.random.standard_normal((N, N_CH, H)))
    f_input = bf(np.random.standard_normal((N, H)))
    iou_input = bf(np.random.standard_normal((N, 3 * H)) * 0.5)
    U_f0 = bf(np.random.standard_normal((D, H, H)) * 0.8 / np.sqrt(H))
    U_iou0 = bf(np.random.standard_normal((D, 3 * H, H)) * 1.6 / np.sqrt(D * H))
    g = bf(np.random.standard_normal((2, N, H)) * np.exp2(np.random.randint(-6, 1, (1, N, 1))) * 8.0 / s[None, :, None] * u[None, None, :])
    nh = f64(nh0)
    f_logits = (nh.transpose(1, 0, 2) @ f64(U_f0).transpose(0, 2, 1)).transpose(1, 0, 2) + f64(f_input)[:, None, :]
    iou = nh.reshape(N, D * H) @ f64(U_iou0).transpose(0, 2, 1).reshape(D * H, 3 * H) + 2.0 * f64(iou_input)
    i, o, uu = np.split(iou, 3, axis=1)
    c = sigmoid(i) * np.tanh(uu) + np.sum(sigmoid(f_logits) * f64(neighbour_c), axis=1)
    return {
        "neighbour_h": bf(f64(nh0) * s[:, None, None]),
        "neighbour_c": neighbour_c,
        "f_input": f_input,
        "iou_input": iou_input,
        "U_f": bf(f64(U_f0) / u[None, :, None]),
        "U_iou": bf(f64(U_iou0) / np.tile(u, 3)[None, :, None]),
        "f_logits": np.asarray(f_logits, np.float32),
        "iou": np.asarray(iou, np.float32),
        "c": np.asarray(c, np.float32),
        "grad_out": g,
    }


def reference(neighbour_h, neighbour_c, f_input, iou_input, U_f, U_iou, f_logits, iou, c, grad_out):
    g = f64(grad_out)
    gh, gc = g[0], g[1]
    i, o, u = np.split(f64(iou), 3, axis=1)
    si, so, tu, tc = sigmoid(i), sigmoid(o), np.tanh(u), np.tanh(f64(c))
    dc = gc + gh * so * (1.0 - tc * tc)
    di = dc * tu * si * (1.0 - si)
    do = gh * tc * so * (1.0 - so)
    du = dc * si * (1.0 - tu * tu)
    diou = np.concatenate([di, do, du], axis=1)
    f = sigmoid(f64(f_logits))
    df = dc[:, None, :] * f64(neighbour_c) * f * (1.0 - f)
    part_f = mxq(df.transpose(1, 0, 2), 2, "e5m2") @ mxq(f64(U_f), 1, "e4m3")
    w_iou = f64(U_iou).transpose(1, 0, 2).reshape(3 * H, D * H)
    part_iou = mxq(diou, 1, "e5m2") @ mxq(w_iou, 0, "e4m3")
    d_nh = part_f.transpose(1, 0, 2) + part_iou.reshape(N, D, H)
    nh = f64(neighbour_h).reshape(N, D * H)
    dw = mxq(diou, 0, "e5m2").T @ mxq(nh, 0, "e4m3")
    d_U_iou = dw.reshape(3 * H, D, H).transpose(1, 0, 2)
    return d_nh, d_U_iou

@@ -1,0 +1,267 @@
+from contextlib import ExitStack
+
+import concourse.mybir as mybir
+from concourse.masks import make_identity
+
+FLOPS = 2 * 1024 * 1024 * (512 + 1536) + 2 * 1024 * 1536 * 1024
+BYTES = 32 * 1024 * 1024
+
+F32 = mybir.dt.float32
+BF16 = mybir.dt.bfloat16
+U32 = mybir.dt.uint32
+U8 = mybir.dt.uint8
+E4 = mybir.dt.float8_e4m3fn_x4
+E5 = mybir.dt.float8_e5m2_x4
+ACT = mybir.ActivationFunctionType
+ALU = mybir.AluOpType
+
+P = 128
+H = 512
+GATE_COL = {"i": 0, "o": 512, "u": 1024}
+GATE_ROW = {"i": 0, "o": 1, "u": 2}
+
+
+def tile_generictreelstmcell_t_v_kernel(
+    tc, neighbour_h, neighbour_c, f_input, iou_input, U_f, U_iou, f_logits, iou, c, grad_out, out_0, out_1
+):
+    nc = tc.nc
+    iou_v = iou.rearrange("(G p j) w -> G p j w", p=P, j=4)
+    c_v = c.rearrange("(G p j) w -> G p j w", p=P, j=4)
+    fl_v = f_logits.rearrange("(G p j) d w -> G p j d w", p=P, j=4)
+    ncc_v = neighbour_c.rearrange("(G p j) d w -> G p j d w", p=P, j=4)
+    nh_v = neighbour_h.rearrange("(G p j) d w -> G p j (d w)", p=P, j=4)
+    g_v = grad_out.rearrange("s (G p j) w -> G p s j w", p=P, j=4)
+    o0_v = out_0.rearrange("(G p j) d h -> G p j (d h)", p=P, j=4)
+    o1_v = out_1.rearrange("d (t m) h -> t m d h", m=P)
+    ui_v = U_iou.rearrange("d (g p t) h -> d g p t h", p=P, t=4)
+    uf_v = U_f.rearrange("d (p t) h -> d p t h", t=4)
+
+    with ExitStack() as ctx:
+        const = ctx.enter_context(tc.tile_pool(name="const", bufs=1))
+        raw = ctx.enter_context(tc.tile_pool(name="raw", bufs=2))
+        tmp = ctx.enter_context(tc.tile_pool(name="tmp", bufs=2))
+        dzp = ctx.enter_context(tc.tile_pool(name="dzp", bufs=2))
+        wraw = ctx.enter_context(tc.tile_pool(name="wraw", bufs=3))
+        grp = ctx.enter_context(tc.tile_pool(name="grp", bufs=3))
+        keep = ctx.enter_context(tc.tile_pool(name="keep", bufs=1))
+        cbp = ctx.enter_context(tc.tile_pool(name="cbp", bufs=8))
+        outp = ctx.enter_context(tc.tile_pool(name="outp", bufs=3))
+        pst = ctx.enter_context(tc.psum_pool(name="pst", bufs=2))
+        psa = ctx.enter_context(tc.psum_pool(name="psa", bufs=6))
+
+        ident = const.tile([P, P], F32, name="ident")
+        make_identity(nc, ident[:])
+        warm = const.tile([P, 1], F32, name="warm")
+        nc.vector.memset(warm[:], 0.0)
+        nc.scalar.activation(out=warm[:], in_=warm[:], func=ACT.Tanh)
+
+        S = {}
+        DZ = {}
+        CB = {}
+        WC = {}
+        NHC = {}
+        AC = {}
+        NH = {}
+
+        def stt(out, in0, scalar, in1, op0, op1):
+            nc.vector.scalar_tensor_tensor(out=out, in0=in0, scalar=scalar, in1=in1, op0=op0, op1=op1)
+
+        def load_slab(s, split):
+            G, j0 = s // 2, 2 * (s % 2)
+            js = slice(j0, j0 + 2)
+            t = {}
+            t["iou"] = raw.tile([P, 2, 1536], F32, name="iou", tag="iou")
+            t["c"] = raw.tile([P, 2, H], F32, name="c", tag="c")
+            t["g"] = raw.tile([P, 2, 2, H], BF16, name="g", tag="g")
+            t["fl"] = raw.tile([P, 2, 2, H], F32, name="fl", tag="fl")
+            t["ncc"] = raw.tile([P, 2, 2, H], BF16, name="ncc", tag="ncc")
+            S[s] = t
+            if split:
+                nc.sync.dma_start(out=t["iou"][:, :, 512:1024], in_=iou_v[G, :, js, 512:1024])
+                nc.sync.dma_start(out=t["c"][:], in_=c_v[G, :, js, :])
+                nc.sync.dma_start(out=t["g"][:], in_=g_v[G, :, :, js, :])
+                nc.sync.dma_start(out=t["iou"][:, :, 0:512], in_=iou_v[G, :, js, 0:512])
+                nc.sync.dma_start(out=t["iou"][:, :, 1024:1536], in_=iou_v[G, :, js, 1024:1536])
+            else:
+                nc.sync.dma_start(out=t["iou"][:], in_=iou_v[G, :, js, :])
+                nc.sync.dma_start(out=t["c"][:], in_=c_v[G, :, js, :])
+                nc.sync.dma_start(out=t["g"][:], in_=g_v[G, :, :, js, :])
+            nc.sync.dma_start(out=t["fl"][:], in_=fl_v[G, :, js, :, :])
+            nc.sync.dma_start(out=t["ncc"][:], in_=ncc_v[G, :, js, :, :])
+
+        def gate(s, x):
+            return S[s]["iou"][:, :, GATE_COL[x]:GATE_COL[x] + H]
+
+        def act_c(s):
+            t = S[s]
+            nc.scalar.activation(out=gate(s, "o"), in_=gate(s, "o"), func=ACT.Tanh, scale=0.5)
+            nc.scalar.activation(out=t["c"][:], in_=t["c"][:], func=ACT.Tanh)
+            t["tcq"] = tmp.tile([P, 2, H], F32, name="tcq", tag="tcq")
+            nc.scalar.activation(out=t["tcq"][:], in_=t["c"][:], func=ACT.Square, scale=0.5)
+
+        def act_iu(s):
+            t = S[s]
+            nc.scalar.activation(out=gate(s, "i"), in_=gate(s, "i"), func=ACT.Tanh, scale=0.5)
+            nc.scalar.activation(out=gate(s, "u"), in_=gate(s, "u"), func=ACT.Tanh)
+            t["tusq"] = tmp.tile([P, 2, H], F32, name="tusq", tag="tusq")
+            nc.scalar.activation(out=t["tusq"][:], in_=gate(s, "u"), func=ACT.Square)
+
+        def act_f(s):
+            fl = S[s]["fl"][:].rearrange("p j d w -> p (j d w)")
+            nc.scalar.activation(out=fl, in_=fl, func=ACT.Tanh, scale=0.5)
+            nc.scalar.activation(out=fl, in_=fl, func=ACT.Square)
+
+        def dz(s, x):
+            G, j0 = s // 2, 2 * (s % 2)
+            if (G, x) not in DZ:
+                DZ[(G, x)] = dzp.tile([P, 4, H], BF16, name="dz" + x, tag="dz" + x)
+            return DZ[(G, x)][:, j0:j0 + 2, :]
+
+        def v_t3(s):
+            stt(S[s]["c"][:], gate(s, "o"), -1.0, S[s]["c"][:], ALU.add, ALU.mult)
+
+        def v_p1(s):
+            stt(gate(s, "o"), gate(s, "o"), 1.0, S[s]["g"][:, 0, :, :], ALU.add, ALU.mult)
+
+        def v_q(s):
+            stt(S[s]["tcq"][:], S[s]["tcq"][:], -0.25, gate(s, "o"), ALU.add, ALU.mult)
+
+        def v_dcm(s):
+            stt(S[s]["tcq"][:], S[s]["g"][:, 1, :, :], -0.5, S[s]["tcq"][:], ALU.mult, ALU.add)
+
+        def v_do(s):
+            stt(dz(s, "o"), S[s]["c"][:], -0.25, gate(s, "o"), ALU.mult, ALU.mult)
+
+        def v_t1(s):
+            stt(gate(s, "u"), gate(s, "i"), -1.0, gate(s, "u"), ALU.add, ALU.mult)
+
+        def v_x(s):
+            stt(gate(s, "i"), gate(s, "i"), 1.0, S[s]["tcq"][:], ALU.add, ALU.mult)
+
+        def v_di(s):
+            stt(dz(s, "i"), gate(s, "u"), 0.5, gate(s, "i"), ALU.mult, ALU.mult)
+
+        def v_du(s):
+            stt(dz(s, "u"), S[s]["tusq"][:], -1.0, gate(s, "i"), ALU.add, ALU.mult)
+
+        def v_y(s, d):
+            stt(S[s]["fl"][:, :, d, :], S[s]["fl"][:, :, d, :], -1.0, S[s]["ncc"][:, :, d, :], ALU.add, ALU.mult)
+
+        def v_df(s, d):
+            if "dzf" not in S[s]:
+                S[s]["dzf"] = dzp.tile([P, 2, 2, H], BF16, name="dzf", tag="dzf")
+            stt(S[s]["dzf"][:, d, :, :], S[s]["fl"][:, :, d, :], 0.5, S[s]["tcq"][:], ALU.mult, ALU.mult)
+
+        def copy_on(eng, out, in_):
+            if eng == "v":
+                nc.vector.tensor_copy(out=out, in_=in_)
+            else:
+                nc.scalar.copy(out=out, in_=in_)
+
+        def road_b(s, x, eng):
+            src = S[s]["dzf"][:, int(x[1]), :, :] if x[0] == "f" else dz(s, x)
+            xt = pst.tile([P, 2, 256], F32, name="xt", tag="xt")
+            for jj in range(2):
+                words = src[:, jj, :].bitcast(F32)
+                for u in range(2):
+                    nc.tensor.transpose(xt[:, u, P * jj:P * (jj + 1)], words[:, u:256:2], ident[:])
+            gb = grp.tile([P, 256, 4], BF16, name="gb", tag="gb", align_bytes=64)
+            copy_on(eng, gb[:].bitcast(F32), xt[:].rearrange("q u r -> q r u"))
+            cb = cbp.tile([P, 256], U32, name="cb", tag="cb", align_bytes=64)
+            sb = cbp.tile([P, 256], U8, name="sb", tag="sb", align_bytes=64)
+            nc.vector.quantize_mx(out=cb[:].bitcast(E5), scales=sb[:], in_=gb[:].rearrange("q r t -> q (r t)"))
+            CB[(s, x)] = (cb, sb)
+
+        def iq(src, fmt, eng, name):
+            g4 = grp.tile([P, H, 4], BF16, name="g4", tag="g4", align_bytes=64)
+            copy_on(eng, g4[:], src.rearrange("p t w -> p w t"))
+            cd = keep.tile([P, H], U32, name="c_" + name, align_bytes=64)
+            sc = keep.tile([P, H], U8, name="s_" + name, align_bytes=64)
+            nc.vector.quantize_mx(out=cd[:].bitcast(fmt), scales=sc[:], in_=g4[:].rearrange("p w t -> p (w t)"))
+            return (cd, sc)
+
+        def mx(acc, l, lcols, r, start, stop):
+            nc.tensor.matmul_mx(
+                out=acc[:], lhsT=l[0][:, lcols].bitcast(E5), lhsT_scale=l[1][:, lcols],
+                rhs=r[0][:].bitcast(E4), rhs_scale=r[1][:], start=start, stop=stop,
+            )
+
+        def weights(keys, engs):
+            for (d, x), eng in zip(keys, engs):
+                w = wraw.tile([P, 4, H], BF16, name="w", tag="w")
+                nc.sync.dma_start(out=w[:], in_=uf_v[d] if x == "f" else ui_v[d, GATE_ROW[x]])
+                WC[(d, x)] = iq(w[:], E4, eng, "w%d%s" % (d, x))
+
+        def load_nh(G):
+            NH[G] = wraw.tile([P, 4, 2 * H], BF16, name="nh", tag="nh", bufs=1)
+            nc.sync.dma_start(out=NH[G][:], in_=nh_v[G])
+
+        def nh_codes(G, engs):
+            for d in range(2):
+                NHC[(G, d)] = iq(NH[G][:, :, H * d:H * (d + 1)], E4, engs[d], "nh%d%d" % (G, d))
+
+        def road_a(G, x, eng):
+            AC[(G, x)] = iq(DZ[(G, x)][:], E5, eng, "a%d%s" % (G, x))
+
+        def m0(s, engs):
+            G, j0 = s // 2, 2 * (s % 2)
+            for jj in range(2):
+                o0 = outp.tile([P, 2 * H], F32, name="o0", tag="o0")
+                for d in range(2):
+                    acc = psa.tile([P, H], F32, name="acc", tag="acc")
+                    xs = ["o", "i", "u", "f%d" % d]
+                    for k, x in enumerate(xs):
+                        mx(acc, CB[(s, x)], slice(P * jj, P * (jj + 1)), WC[(d, x[0])], k == 0, k == 3)
+                    copy_on(engs[2 * jj + d], o0[:, H * d:H * (d + 1)], acc[:])
+                nc.sync.dma_start(out=o0_v[G, :, j0 + jj, :], in_=o0[:])
+
+        def m1(x, engs):
+            for jt in range(4):
+                o1 = outp.tile([P, 2, H], F32, name="o1", tag="o1")
+                for d in range(2):
+                    acc = psa.tile([P, H], F32, name="acc", tag="acc")
+                    for G in range(2):
+                        mx(acc, AC[(G, x)], slice(P * jt, P * (jt + 1)), NHC[(G, d)], G == 0, G == 1)
+                    copy_on(engs[2 * jt + d], o1[:, d, :], acc[:])
+                nc.sync.dma_start(out=o1_v[4 * GATE_ROW[x] + jt], in_=o1[:])
+
+        def v_chain_c(s):
+            v_t3(s); v_p1(s); v_q(s); v_dcm(s); v_do(s)
+
+        def v_chain_iu(s):
+            v_t1(s); v_x(s); v_di(s); v_du(s)
+
+        def v_chain_f(s):
+            v_y(s, 0); v_y(s, 1); v_df(s, 0); v_df(s, 1)
+
+        WKEYS = [(d, x) for d in range(2) for x in "oiuf"]
+
+        load_slab(0, True)
+        load_slab(1, False)
+        for s in range(2):
+            act_c(s); v_chain_c(s); road_b(s, "o", "a")
+            act_iu(s); v_chain_iu(s); road_b(s, "i", "a"); road_b(s, "u", "a")
+            act_f(s); v_chain_f(s); road_b(s, "f0", "a"); road_b(s, "f1", "a")
+            if s == 0:
+                weights(WKEYS, "aaavaaav")
+                load_nh(0)
+            m0(s, "aaaa")
+            load_slab(s + 2, False)
+        for x in "oiu":
+            road_a(0, x, "v")
+        nh_codes(0, "vv")
+        load_nh(1)
+        nh_codes(1, "vv")
+        for s in (2, 3):
+            act_c(s); v_chain_c(s); road_b(s, "o", "a")
+        road_a(1, "o", "v")
+        m1("o", "aaaaaaaa")
+        for s in (2, 3):
+            act_iu(s); v_chain_iu(s); road_b(s, "i", "a"); road_b(s, "u", "a")
+        road_a(1, "i", "v")
+        road_a(1, "u", "v")
+        m1("i", "aaaaaaaa")
+        m1("u", "avavavav")
+        for s in (2, 3):
+            act_f(s); v_chain_f(s); road_b(s, "f0", "a"); road_b(s, "f1", "a")
+            m0(s, "avav")

@@ -17,8 +17,62 @@ ALU = mybir.AluOpType
 
 P = 128
 H = 512
-GATE_COL = {"i": 0, "o": 512, "u": 1024}
 GATE_ROW = {"i": 0, "o": 1, "u": 2}
+MANUAL = True
+ORDER = [
+    "ld.0.o.0", "ld.0.c.0", "ld.0.g", "ld.0.o.1", "ld.0.c.1", "ld.0.i", "ld.0.u", "ld.0.f0", "ld.0.f1", "ld.0.ncc",
+    "ld.1.o", "ld.1.c", "ld.1.g", "ld.w0", "ld.w1", "ld.w2", "ld.1.i", "ld.1.u", "ld.1.f0", "ld.1.f1", "ld.1.ncc",
+    "ld.nh0", "ld.2.o", "ld.2.c", "a.to.0.0", "a.tc.0.0", "a.tcq.0.0", "v.t3.0.0", "v.p1.0.0", "a.to.0.1",
+    "a.tc.0.1", "v.q.0.0", "a.tcq.0.1", "v.do.0.0", "a.ti.0", "v.t3.0.1", "v.dcm.0.0", "a.tu.0", "v.p1.0.1",
+    "v.q.0.1", "a.tusq.0", "v.do.0.1", "a.tf0.0", "v.dcm.0.1", "ld.2.i", "tr.0.o", "v.t1.0.0", "ld.2.g", "a.tf1.0",
+    "v.t1.0.1", "v.x.0.0", "a.tfsq0.0", "v.x.0.1", "v.di.0.0", "a.tfsq1.0", "v.di.0.1", "v.du.0.0", "ld.2.f0",
+    "tr.0.i", "a.to.1", "v.du.0.1", "v.y0.0.0", "ld.2.u", "a.tc.1", "v.y1.0.0", "a.tcq.1", "v.df0.0.0", "ld.2.ncc",
+    "ev.0.o", "ev.0.i", "bq.0.o", "ld.2.f1", "v.df1.0.0", "tr.0.u", "ii.w0o", "tr.0.f0", "bq.0.i", "ld.3.o",
+    "v.t3.1.0", "v.t3.1.1", "v.p1.1.0", "a.ti.1", "ld.w3", "iq.w0o", "v.p1.1.1", "a.tu.1", "m0o.0.0.0",
+    "m0o.0.1.0", "v.q.1.0", "v.q.1.1", "a.tusq.1", "v.dcm.1.0", "ev.0.u", "v.dcm.1.1", "a.tf0.1", "v.do.1.0",
+    "ld.3.g", "bq.0.u", "tr.0.f1", "v.do.1.1", "a.tf1.1", "v.t1.1.0", "ld.3.c", "v.t1.1.1", "a.tfsq0.1", "v.x.1.0",
+    "v.x.1.1", "a.tfsq1.1", "v.di.1.0", "v.di.1.1", "ii.w0i", "v.du.1.0", "ld.3.i", "v.du.1.1", "v.y0.1.0",
+    "ii.w0u", "ld.w4", "iq.w0i", "v.y1.1.0", "m0i.0.0.0", "m0i.0.1.0", "v.df0.1.0", "ld.3.ncc", "ev.0.f0", "ld.w5",
+    "iq.w0u", "ld.3.u", "ev.0.f1", "bq.0.f0", "a.to.2", "tr.1.o", "bq.0.f1", "v.df1.1.0", "tr.1.i", "m0u.0.0.0",
+    "a.tc.2", "m0u.0.1.0", "ld.3.f0", "a.tcq.2", "ii.w0f", "ev.1.o", "a.ti.2", "bq.1.o", "ld.w6", "tr.1.u",
+    "iq.w0f", "m0o.1.0.0", "a.tu.2", "v.t3.2.0", "m0f.0.0.0", "m0f.0.1.0", "v.t3.2.1", "m0e.0.0.0", "v.p1.2.0",
+    "m0e.0.1.0", "m0o.1.1.0", "v.p1.2.1", "a.tusq.2", "v.q.2.0", "v.q.2.1", "ii.w1o", "v.dcm.2.0", "v.dcm.2.1",
+    "v.do.2.0", "v.do.2.1", "v.t1.2.0", "ld.3.f1", "ii.w1i", "ld.w7", "iq.w1o", "v.t1.2.1", "m0o.0.0.1",
+    "m0o.0.1.1", "v.x.2.0", "m0o.1.0.1", "v.x.2.1", "ev.1.i", "iq.w1i", "ii.w1u", "bq.1.i", "ii.nh00", "tr.1.f0",
+    "m0i.0.0.1", "m0i.0.1.1", "m0i.1.0.0", "m0i.1.0.1", "v.di.2.0", "m0i.1.1.0", "ii.w1f", "ev.1.u", "a.tf0.2",
+    "tr.1.f1", "iq.w1u", "a.tf1.2", "iq.w1f", "m0u.0.0.1", "m0u.0.1.1", "iq.nh00", "m0f.0.0.1", "a.tfsq0.2",
+    "m0f.0.1.1", "ii.nh01", "m0e.0.0.1", "bq.1.u", "m0e.0.1.1", "ld.nh1", "m0o.1.1.1", "m0s.0.0", "iq.nh01",
+    "m0u.1.0.0", "a.tfsq1.2", "m0s.0.1", "m0u.1.0.1", "v.di.2.1", "m0u.1.1.0", "m0i.1.1.1", "ii.a0o", "m0u.1.1.1",
+    "ev.1.f0", "ev.1.f1", "a.to.3", "bq.1.f0", "tr.2.o", "bq.1.f1", "tr.2.i", "iq.a0o", "m0f.1.0.0", "a.tc.3",
+    "m0f.1.0.1", "v.du.2.0", "m0f.1.1.0", "m0f.1.1.1", "v.du.2.1", "m0e.1.0.0", "v.y0.2.0", "m0e.1.0.1",
+    "m0e.1.1.0", "m0s.1.0", "v.y1.2.0", "m0e.1.1.1", "m1a.o.0.0", "ii.nh10", "m0s.1.1", "m1a.o.0.1", "v.df0.2.0",
+    "v.df1.2.0", "ii.nh11", "iq.nh10", "ii.a0i", "iq.a0i", "a.tcq.3", "iq.nh11", "ii.a0u", "ev.2.o", "a.ti.3",
+    "tr.2.u", "bq.2.o", "a.tu.3", "iq.a0u", "m0o.2.0.0", "m0o.2.0.1", "v.t3.3.0", "m0o.2.1.0", "a.tusq.3",
+    "m0o.2.1.1", "v.t3.3.1", "v.p1.3.0", "ev.2.i", "v.p1.3.1", "ev.2.u", "bq.2.i", "a.tf0.3", "tr.2.f0", "v.q.3.0",
+    "tr.2.f1", "bq.2.u", "m0i.2.0.0", "v.q.3.1", "a.tf1.3", "m0u.2.0.0", "m0i.2.0.1", "v.dcm.3.0", "m0u.2.0.1",
+    "m0i.2.1.0", "v.dcm.3.1", "a.tfsq0.3", "m0u.2.1.0", "m0i.2.1.1", "v.do.3.0", "m0u.2.1.1", "v.do.3.1",
+    "a.tfsq1.3", "v.t1.3.0", "ii.a1o", "ev.2.f0", "ev.2.f1", "tr.3.o", "bq.2.f0", "ev.3.o", "bq.2.f1", "m0f.2.0.0",
+    "iq.a1o", "m0f.2.0.1", "m0e.2.0.0", "m0f.2.1.0", "bq.3.o", "m0f.2.1.1", "m0e.2.0.1", "v.t1.3.1", "m1b.o.0.0",
+    "m1b.o.0.1", "m0e.2.1.0", "m0s.2.0", "v.x.3.0", "m1a.o.1.0", "m1b.o.1.0", "m0e.2.1.1", "v.x.3.1", "m1a.o.1.1",
+    "m1b.o.1.1", "m1e.o.0.0", "m0s.2.1", "v.du.3.0", "m1a.o.2.0", "m1b.o.2.0", "m1e.o.0.1", "v.du.3.1",
+    "m1a.o.2.1", "m1b.o.2.1", "m1e.o.1.0", "m1s.o.0", "v.di.3.0", "m1a.o.3.0", "m1b.o.3.0", "m1e.o.1.1", "ii.a1u",
+    "m1a.o.3.1", "m1b.o.3.1", "m1e.o.2.0", "m1s.o.1", "m1a.u.0.0", "m1e.o.2.1", "m1a.u.0.1", "m1a.u.1.0",
+    "v.di.3.1", "m1e.o.3.0", "m1s.o.2", "iq.a1u", "tr.3.u", "m1e.o.3.1", "ii.a1i", "tr.3.i", "ev.3.u", "m1s.o.3",
+    "m1b.u.0.0", "m1b.u.0.1", "ev.3.i", "m1b.u.1.0", "m1a.u.1.1", "m1e.u.0.0", "bq.3.u", "m1b.u.1.1", "bq.3.i",
+    "m1a.u.2.0", "m1e.u.0.1", "iq.a1i", "m1b.u.2.0", "m1a.u.2.1", "m1e.u.1.0", "m1s.u.0", "m1b.u.2.1", "v.y0.3.0",
+    "m1a.u.3.0", "m1e.u.1.1", "m1b.u.3.0", "m1e.u.2.0", "m1a.u.3.1", "m1s.u.1", "m1b.u.3.1", "v.y1.3.0",
+    "m1e.u.2.1", "m0o.3.0.0", "m0i.3.0.0", "m1e.u.3.0", "m0u.3.0.0", "m1s.u.2", "v.df0.3.0", "m0o.3.0.1",
+    "m1e.u.3.1", "m0i.3.0.1", "m0u.3.0.1", "m0o.3.1.0", "m1s.u.3", "v.df1.3.0", "m0i.3.1.0", "m0u.3.1.0",
+    "m0o.3.1.1", "m0i.3.1.1", "m0u.3.1.1", "m1a.i.0.0", "m1b.i.0.0", "m1a.i.0.1", "m1e.i.0.0", "m1b.i.0.1",
+    "m1e.i.0.1", "tr.3.f0", "m1s.i.0", "ev.3.f0", "tr.3.f1", "m1a.i.3.0", "ev.3.f1", "bq.3.f0", "m1b.i.3.0",
+    "m0f.3.0.0", "bq.3.f1", "m1e.i.3.0", "m0f.3.1.0", "m0f.3.0.1", "m0e.3.0.0", "m0f.3.1.1", "m0e.3.0.1",
+    "m1a.i.3.1", "m0e.3.1.0", "m1a.i.1.0", "m0e.3.1.1", "m0s.3.0", "m1b.i.1.0", "m1a.i.1.1", "m1e.i.1.0",
+    "m0s.3.1", "m1b.i.1.1", "m1a.i.2.0", "m1e.i.1.1", "m1b.i.2.0", "m1a.i.2.1", "m1e.i.2.0", "m1s.i.1",
+    "m1b.i.2.1", "m1b.i.3.1", "m1e.i.2.1", "m1e.i.3.1", "m1s.i.2", "m1s.i.3",
+]
+HOOK = None
+CFG = dict(r4=15, b4=4, tcq=2, tusq=2, dz=2, g4=3, gb=3, w=3, o0=2, o1=2, xt=2, acc=6,
+           w_eng="aaavaaav", nh_eng="vvaa", ra_eng="vvvvvv", m0_eng=["aaaa", "aaaa", "aaaa", "avav"], m1_eng=dict(o="aaaaaaaa", u="aaaaaaaa", i="avavavav"), plan="slab", w_split=4)
 
 
 def tile_generictreelstmcell_t_v_kernel(
@@ -39,15 +93,11 @@ def tile_generictreelstmcell_t_v_kernel(
     with ExitStack() as ctx:
         const = ctx.enter_context(tc.tile_pool(name="const", bufs=1))
         raw = ctx.enter_context(tc.tile_pool(name="raw", bufs=2))
-        tmp = ctx.enter_context(tc.tile_pool(name="tmp", bufs=2))
-        dzp = ctx.enter_context(tc.tile_pool(name="dzp", bufs=2))
-        wraw = ctx.enter_context(tc.tile_pool(name="wraw", bufs=3))
-        grp = ctx.enter_context(tc.tile_pool(name="grp", bufs=3))
         keep = ctx.enter_context(tc.tile_pool(name="keep", bufs=1))
-        cbp = ctx.enter_context(tc.tile_pool(name="cbp", bufs=8))
-        outp = ctx.enter_context(tc.tile_pool(name="outp", bufs=3))
-        pst = ctx.enter_context(tc.psum_pool(name="pst", bufs=2))
-        psa = ctx.enter_context(tc.psum_pool(name="psa", bufs=6))
+        pst = ctx.enter_context(tc.psum_pool(name="pst", bufs=CFG["xt"]))
+        psa = ctx.enter_context(tc.psum_pool(name="psa", bufs=CFG["acc"]))
+        if MANUAL:
+            ctx.enter_context(tc.manual_schedule())
 
         ident = const.tile([P, P], F32, name="ident")
         make_identity(nc, ident[:])
@@ -55,102 +105,89 @@ def tile_generictreelstmcell_t_v_kernel(
         nc.vector.memset(warm[:], 0.0)
         nc.scalar.activation(out=warm[:], in_=warm[:], func=ACT.Tanh)
 
-        S = {}
-        DZ = {}
-        CB = {}
-        WC = {}
-        NHC = {}
-        AC = {}
-        NH = {}
+        T = {}
+        prog = []
+
+        def step(label, fn, *args):
+            prog.append((label, fn, args))
+
+        def rot(key, shape, dtype, tag, **kw):
+            T[key] = raw.tile(shape, dtype, name=tag, tag=tag, bufs=CFG[tag], **kw)
+            return T[key]
 
         def stt(out, in0, scalar, in1, op0, op1):
             nc.vector.scalar_tensor_tensor(out=out, in0=in0, scalar=scalar, in1=in1, op0=op0, op1=op1)
 
-        def load_slab(s, split):
-            G, j0 = s // 2, 2 * (s % 2)
-            js = slice(j0, j0 + 2)
-            t = {}
-            t["iou"] = raw.tile([P, 2, 1536], F32, name="iou", tag="iou")
-            t["c"] = raw.tile([P, 2, H], F32, name="c", tag="c")
-            t["g"] = raw.tile([P, 2, 2, H], BF16, name="g", tag="g")
-            t["fl"] = raw.tile([P, 2, 2, H], F32, name="fl", tag="fl")
-            t["ncc"] = raw.tile([P, 2, 2, H], BF16, name="ncc", tag="ncc")
-            S[s] = t
-            if split:
-                nc.sync.dma_start(out=t["iou"][:, :, 512:1024], in_=iou_v[G, :, js, 512:1024])
-                nc.sync.dma_start(out=t["c"][:], in_=c_v[G, :, js, :])
-                nc.sync.dma_start(out=t["g"][:], in_=g_v[G, :, :, js, :])
-                nc.sync.dma_start(out=t["iou"][:, :, 0:512], in_=iou_v[G, :, js, 0:512])
-                nc.sync.dma_start(out=t["iou"][:, :, 1024:1536], in_=iou_v[G, :, js, 1024:1536])
+        def where(s):
+            return s // 2, slice(2 * (s % 2), 2 * (s % 2) + 2)
+
+        def load_half(s, x, k):
+            G, js = where(s)
+            if k == 0:
+                rot((s, x), [P, 2, H], F32, "r4")
+            j = 2 * (s % 2) + k
+            src = c_v[G, :, j:j + 1, :] if x == "c" else iou_v[G, :, j:j + 1, H * GATE_ROW[x]:H * GATE_ROW[x] + H]
+            nc.sync.dma_start(out=T[(s, x)][:, k:k + 1, :], in_=src)
+
+        def load(s, x):
+            G, js = where(s)
+            if x in GATE_ROW:
+                c0 = H * GATE_ROW[x]
+                nc.sync.dma_start(out=rot((s, x), [P, 2, H], F32, "r4")[:], in_=iou_v[G, :, js, c0:c0 + H])
+            elif x == "c":
+                nc.sync.dma_start(out=rot((s, x), [P, 2, H], F32, "r4")[:], in_=c_v[G, :, js, :])
+            elif x == "g":
+                nc.sync.dma_start(out=rot((s, x), [P, 2, 2, H], BF16, "b4")[:], in_=g_v[G, :, :, js, :])
+            elif x == "ncc":
+                nc.sync.dma_start(out=rot((s, x), [P, 2, 2, H], BF16, "b4")[:], in_=ncc_v[G, :, js, :, :])
             else:
-                nc.sync.dma_start(out=t["iou"][:], in_=iou_v[G, :, js, :])
-                nc.sync.dma_start(out=t["c"][:], in_=c_v[G, :, js, :])
-                nc.sync.dma_start(out=t["g"][:], in_=g_v[G, :, :, js, :])
-            nc.sync.dma_start(out=t["fl"][:], in_=fl_v[G, :, js, :, :])
-            nc.sync.dma_start(out=t["ncc"][:], in_=ncc_v[G, :, js, :, :])
+                nc.sync.dma_start(out=rot((s, x), [P, 2, H], F32, "r4")[:], in_=fl_v[G, :, js, int(x[1]), :])
 
-        def gate(s, x):
-            return S[s]["iou"][:, :, GATE_COL[x]:GATE_COL[x] + H]
+        def act(out, in_, func, scale=1.0):
+            nc.scalar.activation(out=out, in_=in_, func=func, scale=scale)
 
-        def act_c(s):
-            t = S[s]
-            nc.scalar.activation(out=gate(s, "o"), in_=gate(s, "o"), func=ACT.Tanh, scale=0.5)
-            nc.scalar.activation(out=t["c"][:], in_=t["c"][:], func=ACT.Tanh)
-            t["tcq"] = tmp.tile([P, 2, H], F32, name="tcq", tag="tcq")
-            nc.scalar.activation(out=t["tcq"][:], in_=t["c"][:], func=ACT.Square, scale=0.5)
+        def a_tanh(s, x, scale, h=slice(0, 2)):
+            act(T[(s, x)][:, h, :], T[(s, x)][:, h, :], ACT.Tanh, scale)
 
-        def act_iu(s):
-            t = S[s]
-            nc.scalar.activation(out=gate(s, "i"), in_=gate(s, "i"), func=ACT.Tanh, scale=0.5)
-            nc.scalar.activation(out=gate(s, "u"), in_=gate(s, "u"), func=ACT.Tanh)
-            t["tusq"] = tmp.tile([P, 2, H], F32, name="tusq", tag="tusq")
-            nc.scalar.activation(out=t["tusq"][:], in_=gate(s, "u"), func=ACT.Square)
-
-        def act_f(s):
-            fl = S[s]["fl"][:].rearrange("p j d w -> p (j d w)")
-            nc.scalar.activation(out=fl, in_=fl, func=ACT.Tanh, scale=0.5)
-            nc.scalar.activation(out=fl, in_=fl, func=ACT.Square)
+        def a_sq(s, x, new, scale, h=slice(0, 2)):
+            if new:
+                if (s, new) not in T:
+                    rot((s, new), [P, 2, H], F32, new)
+                act(T[(s, new)][:, h, :], T[(s, x)][:, h, :], ACT.Square, scale)
+            else:
+                act(T[(s, x)][:], T[(s, x)][:], ACT.Square, scale)
 
         def dz(s, x):
-            G, j0 = s // 2, 2 * (s % 2)
-            if (G, x) not in DZ:
-                DZ[(G, x)] = dzp.tile([P, 4, H], BF16, name="dz" + x, tag="dz" + x)
-            return DZ[(G, x)][:, j0:j0 + 2, :]
+            G, js = where(s)
+            if ("dz", G, x) not in T:
+                tg = "dz" if CFG["plan"] == "stage2" else "dz" + x
+                T[("dz", G, x)] = raw.tile([P, 4, H], BF16, name=tg, tag=tg, bufs=CFG["dz"])
+            return T[("dz", G, x)][:, js, :]
 
-        def v_t3(s):
-            stt(S[s]["c"][:], gate(s, "o"), -1.0, S[s]["c"][:], ALU.add, ALU.mult)
+        def dzf(s, d):
+            if ("dzf", s) not in T:
+                T[("dzf", s)] = raw.tile([P, 2, 2, H], BF16, name="dzf", tag="dzf", bufs=2)
+            return T[("dzf", s)][:, d, :, :]
 
-        def v_p1(s):
-            stt(gate(s, "o"), gate(s, "o"), 1.0, S[s]["g"][:, 0, :, :], ALU.add, ALU.mult)
+        def t(s, x, h):
+            return T[(s, x)][:, h, :]
 
-        def v_q(s):
-            stt(S[s]["tcq"][:], S[s]["tcq"][:], -0.25, gate(s, "o"), ALU.add, ALU.mult)
-
-        def v_dcm(s):
-            stt(S[s]["tcq"][:], S[s]["g"][:, 1, :, :], -0.5, S[s]["tcq"][:], ALU.mult, ALU.add)
-
-        def v_do(s):
-            stt(dz(s, "o"), S[s]["c"][:], -0.25, gate(s, "o"), ALU.mult, ALU.mult)
-
-        def v_t1(s):
-            stt(gate(s, "u"), gate(s, "i"), -1.0, gate(s, "u"), ALU.add, ALU.mult)
-
-        def v_x(s):
-            stt(gate(s, "i"), gate(s, "i"), 1.0, S[s]["tcq"][:], ALU.add, ALU.mult)
-
-        def v_di(s):
-            stt(dz(s, "i"), gate(s, "u"), 0.5, gate(s, "i"), ALU.mult, ALU.mult)
-
-        def v_du(s):
-            stt(dz(s, "u"), S[s]["tusq"][:], -1.0, gate(s, "i"), ALU.add, ALU.mult)
-
-        def v_y(s, d):
-            stt(S[s]["fl"][:, :, d, :], S[s]["fl"][:, :, d, :], -1.0, S[s]["ncc"][:, :, d, :], ALU.add, ALU.mult)
-
-        def v_df(s, d):
-            if "dzf" not in S[s]:
-                S[s]["dzf"] = dzp.tile([P, 2, 2, H], BF16, name="dzf", tag="dzf")
-            stt(S[s]["dzf"][:, d, :, :], S[s]["fl"][:, :, d, :], 0.5, S[s]["tcq"][:], ALU.mult, ALU.mult)
+        def v_op(name, s, h):
+            if name == "t3": stt(t(s, "c", h), t(s, "o", h), -1.0, t(s, "c", h), ALU.add, ALU.mult)
+            if name == "p1": stt(t(s, "o", h), t(s, "o", h), 1.0, T[(s, "g")][:, 0, h, :], ALU.add, ALU.mult)
+            if name == "q": stt(t(s, "tcq", h), t(s, "tcq", h), -0.25, t(s, "o", h), ALU.add, ALU.mult)
+            if name == "dcm": stt(t(s, "tcq", h), T[(s, "g")][:, 1, h, :], -0.5, t(s, "tcq", h), ALU.mult, ALU.add)
+            if name == "do": stt(dz(s, "o")[:, h, :], t(s, "c", h), -0.25, t(s, "o", h), ALU.mult, ALU.mult)
+            if name == "t1": stt(t(s, "u", h), t(s, "i", h), -1.0, t(s, "u", h), ALU.add, ALU.mult)
+            if name == "x": stt(t(s, "i", h), t(s, "i", h), 1.0, t(s, "tcq", h), ALU.add, ALU.mult)
+            if name == "di": stt(dz(s, "i")[:, h, :], t(s, "u", h), 0.5, t(s, "i", h), ALU.mult, ALU.mult)
+            if name == "du": stt(dz(s, "u")[:, h, :], t(s, "tusq", h), -1.0, t(s, "i", h), ALU.add, ALU.mult)
+            if name in ("y0", "y1"):
+                d = int(name[1])
+                stt(t(s, "f%d" % d, h), t(s, "f%d" % d, h), -1.0, T[(s, "ncc")][:, h, d, :], ALU.add, ALU.mult)
+            if name in ("df0", "df1"):
+                d = int(name[2])
+                stt(dzf(s, d)[:, h, :], t(s, "f%d" % d, h), 0.5, t(s, "tcq", h), ALU.mult, ALU.mult)
 
         def copy_on(eng, out, in_):
             if eng == "v":
@@ -158,27 +195,50 @@ def tile_generictreelstmcell_t_v_kernel(
             else:
                 nc.scalar.copy(out=out, in_=in_)
 
-        def road_b(s, x, eng):
-            src = S[s]["dzf"][:, int(x[1]), :, :] if x[0] == "f" else dz(s, x)
+        def b_tr(s, x):
+            src = dzf(s, int(x[1])) if x[0] == "f" else dz(s, x)
             xt = pst.tile([P, 2, 256], F32, name="xt", tag="xt")
             for jj in range(2):
                 words = src[:, jj, :].bitcast(F32)
                 for u in range(2):
                     nc.tensor.transpose(xt[:, u, P * jj:P * (jj + 1)], words[:, u:256:2], ident[:])
-            gb = grp.tile([P, 256, 4], BF16, name="gb", tag="gb", align_bytes=64)
-            copy_on(eng, gb[:].bitcast(F32), xt[:].rearrange("q u r -> q r u"))
-            cb = cbp.tile([P, 256], U32, name="cb", tag="cb", align_bytes=64)
-            sb = cbp.tile([P, 256], U8, name="sb", tag="sb", align_bytes=64)
-            nc.vector.quantize_mx(out=cb[:].bitcast(E5), scales=sb[:], in_=gb[:].rearrange("q r t -> q (r t)"))
-            CB[(s, x)] = (cb, sb)
+            T[("xt", s, x)] = xt
 
-        def iq(src, fmt, eng, name):
-            g4 = grp.tile([P, H, 4], BF16, name="g4", tag="g4", align_bytes=64)
-            copy_on(eng, g4[:], src.rearrange("p t w -> p w t"))
-            cd = keep.tile([P, H], U32, name="c_" + name, align_bytes=64)
-            sc = keep.tile([P, H], U8, name="s_" + name, align_bytes=64)
-            nc.vector.quantize_mx(out=cd[:].bitcast(fmt), scales=sc[:], in_=g4[:].rearrange("p w t -> p (w t)"))
-            return (cd, sc)
+        def b_ev(s, x, eng):
+            gb = rot(("gb", s, x), [P, 256, 4], BF16, "gb", align_bytes=64)
+            copy_on(eng, gb[:].bitcast(F32), T[("xt", s, x)][:].rearrange("q u r -> q r u"))
+
+        def b_q(s, x):
+            k = "f" if x[0] == "f" else "g"
+            nb = 4 if x[0] == "f" else 12
+            cb = raw.tile([P, 256], U32, name="cb" + k, tag="cb" + k, bufs=nb, align_bytes=64)
+            sb = raw.tile([P, 256], U8, name="sb" + k, tag="sb" + k, bufs=nb, align_bytes=64)
+            nc.vector.quantize_mx(out=cb[:].bitcast(E5), scales=sb[:], in_=T[("gb", s, x)][:].rearrange("q r t -> q (r t)"))
+            T[("cb", s, x)] = (cb, sb)
+
+        def iq_src(key):
+            if key[0] == "w": return T[key][:]
+            if key[0] == "nh": return T[("nhraw", key[1])][:, :, H * key[2]:H * (key[2] + 1)]
+            return T[("dz", key[1], key[2])][:]
+
+        def iq_i(key, eng):
+            g4 = rot(("g4", key), [P, H, 4], BF16, "g4", align_bytes=64)
+            copy_on(eng, g4[:], iq_src(key).rearrange("p t w -> p w t"))
+
+        def iq_q(key):
+            nm = "%s%s%s" % key
+            cd = keep.tile([P, H], U32, name="c_" + nm, align_bytes=64)
+            sc = keep.tile([P, H], U8, name="s_" + nm, align_bytes=64)
+            fmt = E5 if key[0] == "a" else E4
+            nc.vector.quantize_mx(out=cd[:].bitcast(fmt), scales=sc[:], in_=T[("g4", key)][:].rearrange("p w t -> p (w t)"))
+            T[("cd", key)] = (cd, sc)
+
+        def w_load(d, x):
+            nc.sync.dma_start(out=rot(("w", d, x), [P, 4, H], BF16, "w")[:], in_=uf_v[d] if x == "f" else ui_v[d, GATE_ROW[x]])
+
+        def nh_load(G):
+            T[("nhraw", G)] = raw.tile([P, 4, 2 * H], BF16, name="nh", tag="nh", bufs=1)
+            nc.sync.dma_start(out=T[("nhraw", G)][:], in_=nh_v[G])
 
         def mx(acc, l, lcols, r, start, stop):
             nc.tensor.matmul_mx(
@@ -186,82 +246,268 @@ def tile_generictreelstmcell_t_v_kernel(
                 rhs=r[0][:].bitcast(E4), rhs_scale=r[1][:], start=start, stop=stop,
             )
 
-        def weights(keys, engs):
-            for (d, x), eng in zip(keys, engs):
-                w = wraw.tile([P, 4, H], BF16, name="w", tag="w")
-                nc.sync.dma_start(out=w[:], in_=uf_v[d] if x == "f" else ui_v[d, GATE_ROW[x]])
-                WC[(d, x)] = iq(w[:], E4, eng, "w%d%s" % (d, x))
+        def m0_mm(s, jj, d, xs):
+            if ("acc0", s, jj, d) not in T:
+                T[("acc0", s, jj, d)] = psa.tile([P, H], F32, name="acc", tag="acc")
+            for x in xs:
+                mx(T[("acc0", s, jj, d)], T[("cb", s, x)], slice(P * jj, P * (jj + 1)), T[("cd", ("w", d, x[0]))], x == "o", x[0] == "f")
 
-        def load_nh(G):
-            NH[G] = wraw.tile([P, 4, 2 * H], BF16, name="nh", tag="nh", bufs=1)
-            nc.sync.dma_start(out=NH[G][:], in_=nh_v[G])
+        def m0_ev(s, jj, d, eng):
+            if ("o0", s, jj) not in T:
+                rot(("o0", s, jj), [P, 2 * H], F32, "r4")
+            copy_on(eng, T[("o0", s, jj)][:, H * d:H * (d + 1)], T[("acc0", s, jj, d)][:])
 
-        def nh_codes(G, engs):
-            for d in range(2):
-                NHC[(G, d)] = iq(NH[G][:, :, H * d:H * (d + 1)], E4, engs[d], "nh%d%d" % (G, d))
+        def m0_st(s, jj):
+            G, js = where(s)
+            nc.sync.dma_start(out=o0_v[G, :, 2 * (s % 2) + jj, :], in_=T[("o0", s, jj)][:])
 
-        def road_a(G, x, eng):
-            AC[(G, x)] = iq(DZ[(G, x)][:], E5, eng, "a%d%s" % (G, x))
+        def m1_mm(x, jt, d, G):
+            if G == 0:
+                T[("acc1", x, jt, d)] = psa.tile([P, H], F32, name="acc", tag="acc")
+            acc = T[("acc1", x, jt, d)]
+            mx(acc, T[("cd", ("a", G, x))], slice(P * jt, P * (jt + 1)), T[("cd", ("nh", G, d))], G == 0, G == 1)
 
-        def m0(s, engs):
-            G, j0 = s // 2, 2 * (s % 2)
+        def m1_ev(x, jt, d, eng):
+            if ("o1", x, jt) not in T:
+                rot(("o1", x, jt), [P, 2, H], F32, "r4")
+            copy_on(eng, T[("o1", x, jt)][:, d, :], T[("acc1", x, jt, d)][:])
+
+        def m1_st(x, jt):
+            nc.sync.dma_start(out=o1_v[4 * GATE_ROW[x] + jt], in_=T[("o1", x, jt)][:])
+
+        HALves = (slice(0, 1), slice(1, 2))
+        FULL = (slice(0, 2),)
+
+        def chain(s, names, halves):
+            for n in names:
+                for k, h in enumerate(halves):
+                    step("v.%s.%d.%d" % (n, s, k), v_op, n, s, h)
+
+        def roadb(s, x, eng="a"):
+            step("tr.%d.%s" % (s, x), b_tr, s, x)
+            step("ev.%d.%s" % (s, x), b_ev, s, x, eng)
+            step("bq.%d.%s" % (s, x), b_q, s, x)
+
+        def iq(key, eng):
+            nm = "%s%s%s" % key
+            step("ii." + nm, iq_i, key, eng)
+            step("iq." + nm, iq_q, key)
+
+        def M0(s, pre=True):
             for jj in range(2):
-                o0 = outp.tile([P, 2 * H], F32, name="o0", tag="o0")
                 for d in range(2):
-                    acc = psa.tile([P, H], F32, name="acc", tag="acc")
-                    xs = ["o", "i", "u", "f%d" % d]
-                    for k, x in enumerate(xs):
-                        mx(acc, CB[(s, x)], slice(P * jj, P * (jj + 1)), WC[(d, x[0])], k == 0, k == 3)
-                    copy_on(engs[2 * jj + d], o0[:, H * d:H * (d + 1)], acc[:])
-                nc.sync.dma_start(out=o0_v[G, :, j0 + jj, :], in_=o0[:])
+                    for x in "oiu":
+                        step("m0%s.%d.%d.%d" % (x, s, jj, d), m0_mm, s, jj, d, [x])
 
-        def m1(x, engs):
+        def M0f(s):
+            for jj in range(2):
+                for d in range(2):
+                    step("m0f.%d.%d.%d" % (s, jj, d), m0_mm, s, jj, d, ["f%d" % d])
+                    step("m0e.%d.%d.%d" % (s, jj, d), m0_ev, s, jj, d, CFG["m0_eng"][s][2 * jj + d])
+                step("m0s.%d.%d" % (s, jj), m0_st, s, jj)
+
+        def M1(x):
             for jt in range(4):
-                o1 = outp.tile([P, 2, H], F32, name="o1", tag="o1")
                 for d in range(2):
-                    acc = psa.tile([P, H], F32, name="acc", tag="acc")
-                    for G in range(2):
-                        mx(acc, AC[(G, x)], slice(P * jt, P * (jt + 1)), NHC[(G, d)], G == 0, G == 1)
-                    copy_on(engs[2 * jt + d], o1[:, d, :], acc[:])
-                nc.sync.dma_start(out=o1_v[4 * GATE_ROW[x] + jt], in_=o1[:])
+                    step("m1a.%s.%d.%d" % (x, jt, d), m1_mm, x, jt, d, 0)
+                    step("m1b.%s.%d.%d" % (x, jt, d), m1_mm, x, jt, d, 1)
+                    step("m1e.%s.%d.%d" % (x, jt, d), m1_ev, x, jt, d, CFG["m1_eng"][x][2 * jt + d])
+                step("m1s.%s.%d" % (x, jt), m1_st, x, jt)
 
-        def v_chain_c(s):
-            v_t3(s); v_p1(s); v_q(s); v_dcm(s); v_do(s)
+        def L(s, xs):
+            for x in xs:
+                step("ld.%d.%s" % (s, x), load, s, x)
 
-        def v_chain_iu(s):
-            v_t1(s); v_x(s); v_di(s); v_du(s)
+        def Ac(s):
+            step("a.to.%d" % s, a_tanh, s, "o", 0.5)
+            step("a.tc.%d" % s, a_tanh, s, "c", 1.0)
+            step("a.tcq.%d" % s, a_sq, s, "c", "tcq", 0.5)
 
-        def v_chain_f(s):
-            v_y(s, 0); v_y(s, 1); v_df(s, 0); v_df(s, 1)
+        def Aiu(s):
+            step("a.ti.%d" % s, a_tanh, s, "i", 0.5)
+            step("a.tu.%d" % s, a_tanh, s, "u", 1.0)
+            step("a.tusq.%d" % s, a_sq, s, "u", "tusq", 1.0)
+
+        def Af(s):
+            for d in range(2):
+                step("a.tf%d.%d" % (d, s), a_tanh, s, "f%d" % d, 0.5)
+            for d in range(2):
+                step("a.tfsq%d.%d" % (d, s), a_sq, s, "f%d" % d, None, 1.0)
 
         WKEYS = [(d, x) for d in range(2) for x in "oiuf"]
+        CCH = ["t3", "p1", "q", "dcm", "do"]
+        ICH = ["t1", "x", "di", "du"]
+        FCH = ["y0", "y1", "df0", "df1"]
 
-        load_slab(0, True)
-        load_slab(1, False)
-        for s in range(2):
-            act_c(s); v_chain_c(s); road_b(s, "o", "a")
-            act_iu(s); v_chain_iu(s); road_b(s, "i", "a"); road_b(s, "u", "a")
-            act_f(s); v_chain_f(s); road_b(s, "f0", "a"); road_b(s, "f1", "a")
-            if s == 0:
-                weights(WKEYS, "aaavaaav")
-                load_nh(0)
-            m0(s, "aaaa")
-            load_slab(s + 2, False)
-        for x in "oiu":
-            road_a(0, x, "v")
-        nh_codes(0, "vv")
-        load_nh(1)
-        nh_codes(1, "vv")
-        for s in (2, 3):
-            act_c(s); v_chain_c(s); road_b(s, "o", "a")
-        road_a(1, "o", "v")
-        m1("o", "aaaaaaaa")
-        for s in (2, 3):
-            act_iu(s); v_chain_iu(s); road_b(s, "i", "a"); road_b(s, "u", "a")
-        road_a(1, "i", "v")
-        road_a(1, "u", "v")
-        m1("i", "aaaaaaaa")
-        m1("u", "avavavav")
-        for s in (2, 3):
-            act_f(s); v_chain_f(s); road_b(s, "f0", "a"); road_b(s, "f1", "a")
-            m0(s, "avav")
+        if CFG["plan"] == "stage":
+            L(0, "ocg"); L(1, "ocg"); L(2, "ocg")
+            Ac(0); Ac(1)
+            for s in range(4):
+                chain(s, CCH, HALves)
+                if s + 3 < 4: L(s + 3, "ocg")
+                if s + 2 < 4: Ac(s + 2)
+                roadb(s, "o")
+                if s == 0:
+                    L(0, "iu"); step("ld.nh0", nh_load, 0)
+                if s == 1:
+                    L(1, "iu"); Aiu(0)
+                    iq(("a", 0, "o"), CFG["ra_eng"][0])
+                if s == 2:
+                    Aiu(1)
+                    for d in range(2): iq(("nh", 0, d), CFG["nh_eng"][d])
+                    step("ld.nh1", nh_load, 1)
+                if s == 3:
+                    iq(("a", 1, "o"), CFG["ra_eng"][3])
+                    for d in range(2): iq(("nh", 1, d), CFG["nh_eng"][2 + d])
+            for s in range(4):
+                chain(s, ICH, HALves)
+                if s + 2 < 4:
+                    L(s + 2, "iu"); Aiu(s + 2)
+                if s == 0:
+                    M1("o")
+                    for k in range(3): step("ld.w%d" % k, w_load, *WKEYS[k])
+                roadb(s, "i"); roadb(s, "u")
+                if s == 1:
+                    iq(("a", 0, "i"), CFG["ra_eng"][1]); iq(("a", 0, "u"), CFG["ra_eng"][2])
+                if s >= 2:
+                    L(s - 2, ["f0", "f1", "ncc"]); Af(s - 2)
+                if CFG.get("w_early"):
+                    for k in range(2 * s, 2 * s + 2):
+                        iq(("w",) + WKEYS[k], CFG["w_eng"][k])
+                        if k + 3 < 8: step("ld.w%d" % (k + 3), w_load, *WKEYS[k + 3])
+            iq(("a", 1, "i"), CFG["ra_eng"][4]); iq(("a", 1, "u"), CFG["ra_eng"][5])
+            M1("i"); M1("u")
+            if not CFG.get("w_early"):
+                for k in range(8):
+                    iq(("w",) + WKEYS[k], CFG["w_eng"][k])
+                    if k + 3 < 8: step("ld.w%d" % (k + 3), w_load, *WKEYS[k + 3])
+            for s in range(4):
+                M0(s)
+                chain(s, FCH, FULL)
+                if s + 2 < 4:
+                    L(s + 2, ["f0", "f1", "ncc"]); Af(s + 2)
+                roadb(s, "f0"); roadb(s, "f1")
+                M0f(s)
+
+        if CFG["plan"] == "stage2":
+            HV = HALves
+            step("ld.0.o.0", load_half, 0, "o", 0); step("ld.0.c.0", load_half, 0, "c", 0)
+            L(0, "g")
+            step("ld.0.o.1", load_half, 0, "o", 1); step("ld.0.c.1", load_half, 0, "c", 1)
+            L(1, "ocg"); L(2, "ocg")
+            for k, h in enumerate(HV):
+                step("a.to.0.%d" % k, a_tanh, 0, "o", 0.5, h)
+                step("a.tc.0.%d" % k, a_tanh, 0, "c", 1.0, h)
+                step("a.tcq.0.%d" % k, a_sq, 0, "c", "tcq", 0.5, h)
+            Ac(1)
+            for s in range(4):
+                if s + 2 < 4: Ac(s + 2)
+                chain(s, CCH, HV)
+                if s + 3 < 4: L(s + 3, "ocg")
+                if s == 0: step("ld.nh0", nh_load, 0)
+                L(s, "iu")
+                roadb(s, "o")
+                if s == 1:
+                    iq(("a", 0, "o"), CFG["ra_eng"][0])
+                    for d in range(2): iq(("nh", 0, d), CFG["nh_eng"][d])
+                    step("ld.nh1", nh_load, 1)
+                if s >= 2: Aiu(s - 2)
+                if s == 2:
+                    for d in range(2): iq(("nh", 1, d), CFG["nh_eng"][2 + d])
+            iq(("a", 1, "o"), CFG["ra_eng"][3])
+            M1("o")
+            for k in range(3): step("ld.w%d" % k, w_load, *WKEYS[k])
+            for s in range(4):
+                if s + 2 < 4: Aiu(s + 2)
+                chain(s, ["t1", "x", "du"], HV)
+                roadb(s, "u")
+                if s == 1: iq(("a", 0, "u"), CFG["ra_eng"][2])
+            iq(("a", 1, "u"), CFG["ra_eng"][5])
+            M1("u")
+            for k in range(CFG["w_split"]):
+                iq(("w",) + WKEYS[k], CFG["w_eng"][k])
+                if k + 3 < 8: step("ld.w%d" % (k + 3), w_load, *WKEYS[k + 3])
+            for s in range(4):
+                chain(s, ["di"], HV)
+                roadb(s, "i")
+                if s == 1: iq(("a", 0, "i"), CFG["ra_eng"][1])
+                if s < 2:
+                    L(s, ["f0", "f1", "ncc"])
+            iq(("a", 1, "i"), CFG["ra_eng"][4])
+            M1("i")
+            for k in range(CFG["w_split"], 8):
+                iq(("w",) + WKEYS[k], CFG["w_eng"][k])
+                if k + 3 < 8: step("ld.w%d" % (k + 3), w_load, *WKEYS[k + 3])
+            Af(0); Af(1)
+            for s in range(4):
+                M0(s)
+                chain(s, FCH, FULL)
+                if s + 2 < 4:
+                    L(s + 2, ["f0", "f1", "ncc"]); Af(s + 2)
+                roadb(s, "f0"); roadb(s, "f1")
+                M0f(s)
+
+        if CFG["plan"] == "slab":
+            HV = HALves
+            step("ld.0.o.0", load_half, 0, "o", 0); step("ld.0.c.0", load_half, 0, "c", 0)
+            L(0, "g")
+            step("ld.0.o.1", load_half, 0, "o", 1); step("ld.0.c.1", load_half, 0, "c", 1)
+            L(0, "iu"); L(0, ["f0", "f1", "ncc"]); L(1, "ocg")
+            for k in range(3): step("ld.w%d" % k, w_load, *WKEYS[k])
+            for k, h in enumerate(HV):
+                step("a.to.0.%d" % k, a_tanh, 0, "o", 0.5, h)
+                step("a.tc.0.%d" % k, a_tanh, 0, "c", 1.0, h)
+                step("a.tcq.0.%d" % k, a_sq, 0, "c", "tcq", 0.5, h)
+            Aiu(0); Af(0)
+            for s in range(4):
+                last = s == 3
+                if s + 1 < 4:
+                    Ac(s + 1)
+                chain(s, CCH, HV)
+                roadb(s, "o")
+                if s + 1 < 4:
+                    L(s + 1, "iu"); Aiu(s + 1)
+                if last:
+                    iq(("a", 1, "o"), CFG["ra_eng"][3]); M1("o")
+                    chain(s, ["t1", "x", "du"], HV)
+                    roadb(s, "u")
+                    iq(("a", 1, "u"), CFG["ra_eng"][5]); M1("u")
+                    chain(s, ["di"], HV)
+                    roadb(s, "i")
+                    iq(("a", 1, "i"), CFG["ra_eng"][4])
+                else:
+                    chain(s, ICH, HV)
+                    roadb(s, "i"); roadb(s, "u")
+                if s + 1 < 4:
+                    L(s + 1, ["f0", "f1", "ncc"]); Af(s + 1)
+                if s == 0:
+                    for k in range(8):
+                        iq(("w",) + WKEYS[k], CFG["w_eng"][k])
+                        if k + 3 < 8: step("ld.w%d" % (k + 3), w_load, *WKEYS[k + 3])
+                    step("ld.nh0", nh_load, 0)
+                M0(s)
+                chain(s, FCH, FULL)
+                if s + 2 < 4:
+                    L(s + 2, "ocg")
+                roadb(s, "f0"); roadb(s, "f1")
+                M0f(s)
+                if last:
+                    M1("i")
+                if s == 0:
+                    for d in range(2): iq(("nh", 0, d), CFG["nh_eng"][d])
+                    step("ld.nh1", nh_load, 1)
+                if s == 1:
+                    for d in range(2): iq(("nh", 1, d), CFG["nh_eng"][2 + d])
+                    for k, x in enumerate("oiu"): iq(("a", 0, x), CFG["ra_eng"][k])
+
+        todo = prog
+        if ORDER is not None:
+            byl = {}
+            for l, fn, args in prog:
+                byl[l] = (l, fn, args)
+            todo = [byl[l] for l in ORDER]
+            assert len(todo) == len(prog)
+        for l, fn, args in todo:
+            if HOOK is not None:
+                HOOK(l)
+            fn(*args)

@@ -20,59 +20,60 @@ H = 512
 GATE_ROW = {"i": 0, "o": 1, "u": 2}
 MANUAL = True
 ORDER = [
-    "ld.0.o.0", "ld.0.c.0", "ld.0.g", "ld.0.o.1", "ld.0.c.1", "ld.0.i", "ld.0.u", "ld.0.f0", "ld.0.f1", "ld.0.ncc",
-    "ld.1.o", "ld.1.c", "ld.1.g", "ld.w0", "ld.w1", "ld.w2", "ld.1.i", "ld.1.u", "ld.1.f0", "ld.1.f1", "ld.1.ncc",
-    "ld.nh0", "ld.2.o", "ld.2.c", "a.to.0.0", "a.tc.0.0", "a.tcq.0.0", "v.t3.0.0", "v.p1.0.0", "a.to.0.1",
-    "a.tc.0.1", "v.q.0.0", "a.tcq.0.1", "v.do.0.0", "a.ti.0", "v.t3.0.1", "v.dcm.0.0", "a.tu.0", "v.p1.0.1",
-    "v.q.0.1", "a.tusq.0", "v.do.0.1", "a.tf0.0", "v.dcm.0.1", "ld.2.i", "tr.0.o", "v.t1.0.0", "ld.2.g", "a.tf1.0",
-    "v.t1.0.1", "v.x.0.0", "a.tfsq0.0", "v.x.0.1", "v.di.0.0", "a.tfsq1.0", "v.di.0.1", "v.du.0.0", "ld.2.f0",
-    "tr.0.i", "a.to.1", "v.du.0.1", "v.y0.0.0", "ld.2.u", "a.tc.1", "v.y1.0.0", "a.tcq.1", "v.df0.0.0", "ld.2.ncc",
-    "ev.0.o", "ev.0.i", "bq.0.o", "ld.2.f1", "v.df1.0.0", "tr.0.u", "ii.w0o", "tr.0.f0", "bq.0.i", "ld.3.o",
-    "v.t3.1.0", "v.t3.1.1", "v.p1.1.0", "a.ti.1", "ld.w3", "iq.w0o", "v.p1.1.1", "a.tu.1", "m0o.0.0.0",
-    "m0o.0.1.0", "v.q.1.0", "v.q.1.1", "a.tusq.1", "v.dcm.1.0", "ev.0.u", "v.dcm.1.1", "a.tf0.1", "v.do.1.0",
-    "ld.3.g", "bq.0.u", "tr.0.f1", "v.do.1.1", "a.tf1.1", "v.t1.1.0", "ld.3.c", "v.t1.1.1", "a.tfsq0.1", "v.x.1.0",
-    "v.x.1.1", "a.tfsq1.1", "v.di.1.0", "v.di.1.1", "ii.w0i", "v.du.1.0", "ld.3.i", "v.du.1.1", "v.y0.1.0",
-    "ii.w0u", "ld.w4", "iq.w0i", "v.y1.1.0", "m0i.0.0.0", "m0i.0.1.0", "v.df0.1.0", "ld.3.ncc", "ev.0.f0", "ld.w5",
-    "iq.w0u", "ld.3.u", "ev.0.f1", "bq.0.f0", "a.to.2", "tr.1.o", "bq.0.f1", "v.df1.1.0", "tr.1.i", "m0u.0.0.0",
-    "a.tc.2", "m0u.0.1.0", "ld.3.f0", "a.tcq.2", "ii.w0f", "ev.1.o", "a.ti.2", "bq.1.o", "ld.w6", "tr.1.u",
-    "iq.w0f", "m0o.1.0.0", "a.tu.2", "v.t3.2.0", "m0f.0.0.0", "m0f.0.1.0", "v.t3.2.1", "m0e.0.0.0", "v.p1.2.0",
-    "m0e.0.1.0", "m0o.1.1.0", "v.p1.2.1", "a.tusq.2", "v.q.2.0", "v.q.2.1", "ii.w1o", "v.dcm.2.0", "v.dcm.2.1",
-    "v.do.2.0", "v.do.2.1", "v.t1.2.0", "ld.3.f1", "ii.w1i", "ld.w7", "iq.w1o", "v.t1.2.1", "m0o.0.0.1",
-    "m0o.0.1.1", "v.x.2.0", "m0o.1.0.1", "v.x.2.1", "ev.1.i", "iq.w1i", "ii.w1u", "bq.1.i", "ii.nh00", "tr.1.f0",
-    "m0i.0.0.1", "m0i.0.1.1", "m0i.1.0.0", "m0i.1.0.1", "v.di.2.0", "m0i.1.1.0", "ii.w1f", "ev.1.u", "a.tf0.2",
-    "tr.1.f1", "iq.w1u", "a.tf1.2", "iq.w1f", "m0u.0.0.1", "m0u.0.1.1", "iq.nh00", "m0f.0.0.1", "a.tfsq0.2",
-    "m0f.0.1.1", "ii.nh01", "m0e.0.0.1", "bq.1.u", "m0e.0.1.1", "ld.nh1", "m0o.1.1.1", "m0s.0.0", "iq.nh01",
-    "m0u.1.0.0", "a.tfsq1.2", "m0s.0.1", "m0u.1.0.1", "v.di.2.1", "m0u.1.1.0", "m0i.1.1.1", "ii.a0o", "m0u.1.1.1",
-    "ev.1.f0", "ev.1.f1", "a.to.3", "bq.1.f0", "tr.2.o", "bq.1.f1", "tr.2.i", "iq.a0o", "m0f.1.0.0", "a.tc.3",
-    "m0f.1.0.1", "v.du.2.0", "m0f.1.1.0", "m0f.1.1.1", "v.du.2.1", "m0e.1.0.0", "v.y0.2.0", "m0e.1.0.1",
-    "m0e.1.1.0", "m0s.1.0", "v.y1.2.0", "m0e.1.1.1", "m1a.o.0.0", "ii.nh10", "m0s.1.1", "m1a.o.0.1", "v.df0.2.0",
-    "v.df1.2.0", "ii.nh11", "iq.nh10", "ii.a0i", "iq.a0i", "a.tcq.3", "iq.nh11", "ii.a0u", "ev.2.o", "a.ti.3",
-    "tr.2.u", "bq.2.o", "a.tu.3", "iq.a0u", "m0o.2.0.0", "m0o.2.0.1", "v.t3.3.0", "m0o.2.1.0", "a.tusq.3",
-    "m0o.2.1.1", "v.t3.3.1", "v.p1.3.0", "ev.2.i", "v.p1.3.1", "ev.2.u", "bq.2.i", "a.tf0.3", "tr.2.f0", "v.q.3.0",
-    "tr.2.f1", "bq.2.u", "m0i.2.0.0", "v.q.3.1", "a.tf1.3", "m0u.2.0.0", "m0i.2.0.1", "v.dcm.3.0", "m0u.2.0.1",
-    "m0i.2.1.0", "v.dcm.3.1", "a.tfsq0.3", "m0u.2.1.0", "m0i.2.1.1", "v.do.3.0", "m0u.2.1.1", "v.do.3.1",
-    "a.tfsq1.3", "v.t1.3.0", "ii.a1o", "ev.2.f0", "ev.2.f1", "tr.3.o", "bq.2.f0", "ev.3.o", "bq.2.f1", "m0f.2.0.0",
-    "iq.a1o", "m0f.2.0.1", "m0e.2.0.0", "m0f.2.1.0", "bq.3.o", "m0f.2.1.1", "m0e.2.0.1", "v.t1.3.1", "m1b.o.0.0",
-    "m1b.o.0.1", "m0e.2.1.0", "m0s.2.0", "v.x.3.0", "m1a.o.1.0", "m1b.o.1.0", "m0e.2.1.1", "v.x.3.1", "m1a.o.1.1",
-    "m1b.o.1.1", "m1e.o.0.0", "m0s.2.1", "v.du.3.0", "m1a.o.2.0", "m1b.o.2.0", "m1e.o.0.1", "v.du.3.1",
-    "m1a.o.2.1", "m1b.o.2.1", "m1e.o.1.0", "m1s.o.0", "v.di.3.0", "m1a.o.3.0", "m1b.o.3.0", "m1e.o.1.1", "ii.a1u",
-    "m1a.o.3.1", "m1b.o.3.1", "m1e.o.2.0", "m1s.o.1", "m1a.u.0.0", "m1e.o.2.1", "m1a.u.0.1", "m1a.u.1.0",
-    "v.di.3.1", "m1e.o.3.0", "m1s.o.2", "iq.a1u", "tr.3.u", "m1e.o.3.1", "ii.a1i", "tr.3.i", "ev.3.u", "m1s.o.3",
-    "m1b.u.0.0", "m1b.u.0.1", "ev.3.i", "m1b.u.1.0", "m1a.u.1.1", "m1e.u.0.0", "bq.3.u", "m1b.u.1.1", "bq.3.i",
-    "m1a.u.2.0", "m1e.u.0.1", "iq.a1i", "m1b.u.2.0", "m1a.u.2.1", "m1e.u.1.0", "m1s.u.0", "m1b.u.2.1", "v.y0.3.0",
-    "m1a.u.3.0", "m1e.u.1.1", "m1b.u.3.0", "m1e.u.2.0", "m1a.u.3.1", "m1s.u.1", "m1b.u.3.1", "v.y1.3.0",
-    "m1e.u.2.1", "m0o.3.0.0", "m0i.3.0.0", "m1e.u.3.0", "m0u.3.0.0", "m1s.u.2", "v.df0.3.0", "m0o.3.0.1",
-    "m1e.u.3.1", "m0i.3.0.1", "m0u.3.0.1", "m0o.3.1.0", "m1s.u.3", "v.df1.3.0", "m0i.3.1.0", "m0u.3.1.0",
-    "m0o.3.1.1", "m0i.3.1.1", "m0u.3.1.1", "m1a.i.0.0", "m1b.i.0.0", "m1a.i.0.1", "m1e.i.0.0", "m1b.i.0.1",
-    "m1e.i.0.1", "tr.3.f0", "m1s.i.0", "ev.3.f0", "tr.3.f1", "m1a.i.3.0", "ev.3.f1", "bq.3.f0", "m1b.i.3.0",
-    "m0f.3.0.0", "bq.3.f1", "m1e.i.3.0", "m0f.3.1.0", "m0f.3.0.1", "m0e.3.0.0", "m0f.3.1.1", "m0e.3.0.1",
-    "m1a.i.3.1", "m0e.3.1.0", "m1a.i.1.0", "m0e.3.1.1", "m0s.3.0", "m1b.i.1.0", "m1a.i.1.1", "m1e.i.1.0",
-    "m0s.3.1", "m1b.i.1.1", "m1a.i.2.0", "m1e.i.1.1", "m1b.i.2.0", "m1a.i.2.1", "m1e.i.2.0", "m1s.i.1",
-    "m1b.i.2.1", "m1b.i.3.1", "m1e.i.2.1", "m1e.i.3.1", "m1s.i.2", "m1s.i.3",
+    "ld.0.o.0", "ld.0.c.0", "ld.0.g", "ld.0.o.1", "ld.0.c.1", "ld.w0", "ld.0.i", "ld.0.u", "ld.0.f0", "a.to.0.0",
+    "ld.w1", "a.tc.0.0", "a.tcq.0.0", "v.t3.0.0", "ld.0.f1", "v.p1.0.0", "ld.w2", "a.to.0.1", "v.q.0.0",
+    "ld.0.ncc", "a.tc.0.1", "v.do.0.0", "a.tcq.0.1", "v.dcm.0.0", "ld.nh0", "ii.w0o", "v.t3.0.1", "v.p1.0.1",
+    "ld.1.o", "v.q.0.1", "v.do.0.1", "a.ti.0", "ld.1.c", "v.dcm.0.1", "tr.0.o", "iq.w0o", "a.tu.0", "ld.w3",
+    "a.tusq.0", "ld.1.g", "a.tf0.0", "v.t1.0.0", "v.t1.0.1", "a.tfsq0.0", "v.x.0.0", "ld.1.i", "v.x.0.1",
+    "a.tf1.0", "v.di.0.0", "ld.1.u", "v.di.0.1", "a.tfsq1.0", "v.du.0.0", "tr.0.i", "v.du.0.1", "ld.1.f0",
+    "ev.0.o", "v.y0.0.0", "ev.0.i", "ii.w0i", "bq.0.o", "tr.0.u", "bq.0.i", "m0o.0.0.0", "v.y1.0.0", "m0o.0.1.0",
+    "ld.1.f1", "v.df0.0.0", "ev.0.u", "iq.w0i", "ii.w0u", "ld.1.ncc", "bq.0.u", "v.df1.0.0", "tr.0.f0",
+    "m0i.0.0.0", "ld.w4", "m0i.0.1.0", "a.to.1", "iq.w0u", "ld.2.o", "ii.w0f", "tr.0.f1", "a.tc.1", "m0u.0.0.0",
+    "m0u.0.1.0", "iq.w0f", "ld.w5", "a.tcq.1", "ev.0.f0", "v.t3.1.0", "ld.2.c", "a.ti.1", "bq.0.f0", "v.t3.1.1",
+    "m0f.0.0.0", "v.p1.1.0", "ev.0.f1", "m0f.0.1.0", "ld.w6", "v.p1.1.1", "a.tu.1", "bq.0.f1", "v.q.1.0", "ld.2.g",
+    "a.tusq.1", "v.q.1.1", "v.dcm.1.0", "a.tf0.1", "ld.2.i", "v.dcm.1.1", "v.do.1.0", "a.tf1.1", "v.do.1.1",
+    "ld.2.u", "v.t1.1.0", "a.tfsq0.1", "tr.1.o", "v.t1.1.1", "v.x.1.0", "ld.2.f0", "a.tfsq1.1", "v.x.1.1",
+    "v.di.1.0", "ii.w1o", "ld.2.f1", "v.di.1.1", "v.du.1.0", "tr.1.i", "v.du.1.1", "ld.2.ncc", "v.y0.1.0",
+    "ii.w1i", "iq.w1o", "ld.3.o", "v.y1.1.0", "m0o.0.0.1", "m0o.0.1.1", "ld.w7", "v.df0.1.0", "ii.w1u", "iq.w1i",
+    "ld.3.c", "v.df1.1.0", "m0i.0.0.1", "m0i.0.1.1", "m0e.0.0.0", "ld.3.g", "ii.nh00", "m0e.0.1.0", "a.to.2",
+    "iq.w1u", "ld.3.i", "iq.nh00", "m0u.0.0.1", "a.tc.2", "ii.nh01", "m0u.0.1.1", "ld.3.u", "a.tcq.2", "iq.nh01",
+    "ev.1.o", "ld.3.f0", "v.t3.2.0", "a.ti.2", "bq.1.o", "ii.a0o", "ld.nh1", "tr.1.u", "a.tu.2", "m0o.1.0.0",
+    "m0o.1.0.1", "v.t3.2.1", "a.tusq.2", "ld.3.ncc", "m0o.1.1.0", "iq.a0o", "v.p1.2.0", "ev.1.i", "v.p1.2.1",
+    "ev.1.u", "ii.w1f", "a.tf0.2", "tr.1.f0", "a.tf1.2", "bq.1.i", "tr.1.f1", "iq.w1f", "m0i.1.0.0", "bq.1.u",
+    "a.tfsq0.2", "m0f.0.0.1", "v.q.2.0", "m0f.0.1.1", "v.q.2.1", "m0e.0.0.1", "m0u.1.0.0", "v.dcm.2.0",
+    "m0i.1.0.1", "m0e.0.1.1", "m0s.0.0", "m0u.1.0.1", "v.dcm.2.1", "m0i.1.1.0", "a.tfsq1.2", "m0u.1.1.0",
+    "v.do.2.0", "m0s.0.1", "m0o.1.1.1", "m0i.1.1.1", "v.do.2.1", "m0u.1.1.1", "ev.1.f0", "v.t1.2.0", "ld.3.f1",
+    "ev.1.f1", "bq.1.f0", "a.to.3", "v.t1.2.1", "tr.2.o", "m0f.1.0.0", "bq.1.f1", "m0f.1.1.0", "v.x.2.0",
+    "m0f.1.0.1", "m0e.1.0.0", "m0f.1.1.1", "v.x.2.1", "m0e.1.0.1", "v.di.2.0", "m0e.1.1.0", "m0s.1.0", "v.di.2.1",
+    "m0e.1.1.1", "m1a.o.0.0", "v.du.2.0", "a.tc.3", "m0s.1.1", "v.du.2.1", "tr.2.i", "v.y0.2.0", "ii.nh10",
+    "m1a.o.0.1", "v.y1.2.0", "v.df0.2.0", "ii.nh11", "iq.nh10", "v.df1.2.0", "ii.a0i", "a.tcq.3", "ev.2.o",
+    "iq.nh11", "a.ti.3", "iq.a0i", "ii.a0u", "tr.2.u", "a.tu.3", "bq.2.o", "a.tusq.3", "iq.a0u", "m0o.2.0.0",
+    "v.t3.3.0", "m0o.2.0.1", "ev.2.i", "v.t3.3.1", "m0o.2.1.0", "ev.2.u", "bq.2.i", "v.p1.3.0", "a.tf0.3",
+    "tr.2.f0", "bq.2.u", "v.p1.3.1", "tr.2.f1", "a.tf1.3", "m0i.2.0.0", "v.q.3.0", "m0u.2.0.0", "v.q.3.1",
+    "a.tfsq0.3", "m0i.2.0.1", "v.dcm.3.0", "m0u.2.0.1", "v.dcm.3.1", "m0i.2.1.0", "a.tfsq1.3", "m0u.2.1.0",
+    "v.do.3.0", "m0o.2.1.1", "m0i.2.1.1", "v.do.3.1", "ev.2.f0", "m0u.2.1.1", "v.t1.3.0", "ev.2.f1", "bq.2.f0",
+    "tr.3.o", "bq.2.f1", "m0f.2.0.0", "ev.3.o", "ii.a1o", "m0f.2.0.1", "m0e.2.0.0", "m0f.2.1.0", "m0f.2.1.1",
+    "m0e.2.0.1", "m1a.o.1.0", "bq.3.o", "m0e.2.1.0", "iq.a1o", "m0s.2.0", "m1a.o.1.1", "m0e.2.1.1", "m1a.o.2.0",
+    "v.t1.3.1", "m1b.o.0.0", "m0s.2.1", "m1b.o.0.1", "v.x.3.0", "m1e.o.0.0", "m1b.o.1.0", "m1b.o.1.1", "v.x.3.1",
+    "m1e.o.0.1", "m1b.o.2.0", "m1a.o.2.1", "v.du.3.0", "m1e.o.1.0", "m1s.o.0", "m1b.o.2.1", "m1a.o.3.0",
+    "v.du.3.1", "m1e.o.1.1", "v.di.3.0", "m1e.o.2.0", "m1b.o.3.0", "m1s.o.1", "ii.a1u", "m1e.o.2.1", "tr.3.u",
+    "m1a.o.3.1", "m1e.o.3.0", "m1s.o.2", "m1b.o.3.1", "ev.3.u", "m1a.u.0.0", "v.di.3.1", "m1a.u.0.1", "m1e.o.3.1",
+    "m1a.u.1.0", "bq.3.u", "iq.a1u", "tr.3.i", "m1s.o.3", "m1a.u.1.1", "ev.3.i", "ii.a1i", "m1a.u.2.0",
+    "m1b.u.0.0", "m1b.u.0.1", "m1e.u.0.0", "m1b.u.1.0", "m1b.u.1.1", "m1e.u.0.1", "bq.3.i", "m1b.u.2.0", "iq.a1i",
+    "m1a.u.2.1", "m1e.u.1.0", "m1s.u.0", "m1b.u.2.1", "v.y0.3.0", "m1a.u.3.0", "m1e.u.1.1", "m1b.u.3.0",
+    "m1a.u.3.1", "m1e.u.2.0", "m1s.u.1", "m1b.u.3.1", "v.y1.3.0", "m0o.3.0.0", "m1e.u.2.1", "m0i.3.0.0",
+    "m0u.3.0.0", "m1e.u.3.0", "m1s.u.2", "m0o.3.0.1", "v.df0.3.0", "m0i.3.0.1", "m1e.u.3.1", "m0u.3.0.1",
+    "m0o.3.1.0", "m1s.u.3", "m0i.3.1.0", "v.df1.3.0", "m0u.3.1.0", "tr.3.f0", "m0o.3.1.1", "ev.3.f0", "bq.3.f0",
+    "tr.3.f1", "m0i.3.1.1", "ev.3.f1", "m0u.3.1.1", "m0f.3.0.0", "bq.3.f1", "m0f.3.1.0", "m0e.3.0.0", "m0f.3.0.1",
+    "m0f.3.1.1", "m0e.3.1.0", "m0e.3.0.1", "m1a.i.0.0", "m1b.i.0.0", "m0e.3.1.1", "m0s.3.0", "m1a.i.0.1",
+    "m1e.i.0.0", "m1b.i.0.1", "m0s.3.1", "m1a.i.1.0", "m1e.i.0.1", "m1b.i.1.0", "m1a.i.1.1", "m1e.i.1.0",
+    "m1s.i.0", "m1b.i.1.1", "m1a.i.2.0", "m1e.i.1.1", "m1b.i.2.0", "m1a.i.2.1", "m1e.i.2.0", "m1s.i.1",
+    "m1b.i.2.1", "m1a.i.3.0", "m1e.i.2.1", "m1b.i.3.0", "m1a.i.3.1", "m1e.i.3.0", "m1s.i.2", "m1b.i.3.1",
+    "m1e.i.3.1", "m1s.i.3",
 ]
 HOOK = None
 CFG = dict(r4=15, b4=4, tcq=2, tusq=2, dz=2, g4=3, gb=3, w=3, o0=2, o1=2, xt=2, acc=6,
-           w_eng="aaavaaav", nh_eng="vvaa", ra_eng="vvvvvv", m0_eng=["aaaa", "aaaa", "aaaa", "avav"], m1_eng=dict(o="aaaaaaaa", u="aaaaaaaa", i="avavavav"), plan="slab", w_split=4)
+           w_eng="aaavaaav", nh_eng="vvaa", ra_eng="vvvvvv", m0_eng=["aaaa", "aaaa", "aaaa", "avav"], m1_eng=dict(o="aaaaaaaa", u="aaaaaaaa", i="avavavav"), plan="slab", w_split=4, wq="g", st_g=2)
 
 
 def tile_generictreelstmcell_t_v_kernel(
@@ -160,7 +161,7 @@ def tile_generictreelstmcell_t_v_kernel(
         def dz(s, x):
             G, js = where(s)
             if ("dz", G, x) not in T:
-                tg = "dz" if CFG["plan"] == "stage2" else "dz" + x
+                tg = "dz" if CFG["plan"] in ("stage2", "stage3") else "dz" + x
                 T[("dz", G, x)] = raw.tile([P, 4, H], BF16, name=tg, tag=tg, bufs=CFG["dz"])
             return T[("dz", G, x)][:, js, :]
 
@@ -234,11 +235,13 @@ def tile_generictreelstmcell_t_v_kernel(
             T[("cd", key)] = (cd, sc)
 
         def w_load(d, x):
-            nc.sync.dma_start(out=rot(("w", d, x), [P, 4, H], BF16, "w")[:], in_=uf_v[d] if x == "f" else ui_v[d, GATE_ROW[x]])
+            q = nc.gpsimd if CFG["wq"] == "g" else nc.sync
+            q.dma_start(out=rot(("w", d, x), [P, 4, H], BF16, "w")[:], in_=uf_v[d] if x == "f" else ui_v[d, GATE_ROW[x]])
 
         def nh_load(G):
             T[("nhraw", G)] = raw.tile([P, 4, 2 * H], BF16, name="nh", tag="nh", bufs=1)
-            nc.sync.dma_start(out=T[("nhraw", G)][:], in_=nh_v[G])
+            q = nc.gpsimd if CFG["wq"] == "g" else nc.sync
+            q.dma_start(out=T[("nhraw", G)][:], in_=nh_v[G])
 
         def mx(acc, l, lcols, r, start, stop):
             nc.tensor.matmul_mx(
@@ -259,7 +262,8 @@ def tile_generictreelstmcell_t_v_kernel(
 
         def m0_st(s, jj):
             G, js = where(s)
-            nc.sync.dma_start(out=o0_v[G, :, 2 * (s % 2) + jj, :], in_=T[("o0", s, jj)][:])
+            q = nc.gpsimd if s < CFG["st_g"] else nc.sync
+            q.dma_start(out=o0_v[G, :, 2 * (s % 2) + jj, :], in_=T[("o0", s, jj)][:])
 
         def m1_mm(x, jt, d, G):
             if G == 0:
@@ -446,6 +450,174 @@ def tile_generictreelstmcell_t_v_kernel(
                     L(s + 2, ["f0", "f1", "ncc"]); Af(s + 2)
                 roadb(s, "f0"); roadb(s, "f1")
                 M0f(s)
+
+        if CFG["plan"] == "slab2":
+            HV = HALves
+            step("ld.0.o.0", load_half, 0, "o", 0); step("ld.0.c.0", load_half, 0, "c", 0)
+            L(0, "g")
+            step("ld.0.o.1", load_half, 0, "o", 1); step("ld.0.c.1", load_half, 0, "c", 1)
+            L(0, "iu"); L(0, ["f0", "f1", "ncc"]); L(1, "ocg")
+            for k in range(3): step("ld.w%d" % k, w_load, *WKEYS[k])
+            for k, h in enumerate(HV):
+                step("a.to.0.%d" % k, a_tanh, 0, "o", 0.5, h)
+                step("a.tc.0.%d" % k, a_tanh, 0, "c", 1.0, h)
+                step("a.tcq.0.%d" % k, a_sq, 0, "c", "tcq", 0.5, h)
+            Aiu(0); Af(0)
+            for s in range(2):
+                Ac(s + 1)
+                chain(s, CCH, HV)
+                roadb(s, "o")
+                L(s + 1, "iu"); Aiu(s + 1)
+                chain(s, ICH, HV)
+                roadb(s, "i"); roadb(s, "u")
+                L(s + 1, ["f0", "f1", "ncc"]); Af(s + 1)
+                if s == 0:
+                    for k in range(8):
+                        iq(("w",) + WKEYS[k], CFG["w_eng"][k])
+                        if k + 3 < 8: step("ld.w%d" % (k + 3), w_load, *WKEYS[k + 3])
+                    step("ld.nh0", nh_load, 0)
+                M0(s)
+                chain(s, FCH, FULL)
+                L(s + 2, "ocg")
+                roadb(s, "f0"); roadb(s, "f1")
+                M0f(s)
+                if s == 0:
+                    for d in range(2): iq(("nh", 0, d), CFG["nh_eng"][d])
+                    step("ld.nh1", nh_load, 1)
+                if s == 1:
+                    for d in range(2): iq(("nh", 1, d), CFG["nh_eng"][2 + d])
+                    iq(("a", 0, "o"), CFG["ra_eng"][0])
+            Ac(3)
+            chain(2, CCH, HV); roadb(2, "o")
+            chain(3, CCH, HV); roadb(3, "o")
+            iq(("a", 1, "o"), CFG["ra_eng"][3]); M1("o")
+            L(3, "iu"); Aiu(3)
+            iq(("a", 0, "u"), CFG["ra_eng"][2]); iq(("a", 0, "i"), CFG["ra_eng"][1])
+            chain(2, ICH, HV); roadb(2, "i"); roadb(2, "u")
+            L(3, ["f0", "f1", "ncc"]); Af(3)
+            M0(2)
+            chain(2, FCH, FULL); roadb(2, "f0"); roadb(2, "f1"); M0f(2)
+            chain(3, ["t1", "x", "du"], HV); roadb(3, "u")
+            iq(("a", 1, "u"), CFG["ra_eng"][5]); M1("u")
+            chain(3, ["di"], HV); roadb(3, "i")
+            iq(("a", 1, "i"), CFG["ra_eng"][4])
+            M0(3)
+            chain(3, FCH, FULL); roadb(3, "f0"); roadb(3, "f1"); M0f(3)
+            M1("i")
+
+        if CFG["plan"] == "stage3":
+            HV = HALves
+            step("ld.0.o.0", load_half, 0, "o", 0); step("ld.0.c.0", load_half, 0, "c", 0)
+            L(0, "g")
+            step("ld.0.o.1", load_half, 0, "o", 1); step("ld.0.c.1", load_half, 0, "c", 1)
+            L(1, "ocg"); L(2, "ocg")
+            for k, h in enumerate(HV):
+                step("a.to.0.%d" % k, a_tanh, 0, "o", 0.5, h)
+                step("a.tc.0.%d" % k, a_tanh, 0, "c", 1.0, h)
+                step("a.tcq.0.%d" % k, a_sq, 0, "c", "tcq", 0.5, h)
+            Ac(1)
+            for s in range(4):
+                if s + 2 < 4: Ac(s + 2)
+                chain(s, CCH, HV)
+                if s + 3 < 4: L(s + 3, "ocg")
+                if s == 0: step("ld.nh0", nh_load, 0)
+                L(s, "iu")
+                roadb(s, "o")
+                if s == 1:
+                    iq(("a", 0, "o"), CFG["ra_eng"][0])
+                    for d in range(2): iq(("nh", 0, d), CFG["nh_eng"][d])
+                    step("ld.nh1", nh_load, 1)
+                if s >= 1: Aiu(s - 1)
+                if s == 2:
+                    for d in range(2): iq(("nh", 1, d), CFG["nh_eng"][2 + d])
+                    for k in range(3): step("ld.w%d" % k, w_load, *WKEYS[k])
+            iq(("a", 1, "o"), CFG["ra_eng"][3])
+            M1("o")
+            Aiu(3)
+            for s in range(4):
+                chain(s, ["t1", "x", "du"], HV)
+                roadb(s, "u")
+                if s == 1: iq(("a", 0, "u"), CFG["ra_eng"][2])
+                for k in range(2 * s, 2 * s + 2):
+                    iq(("w",) + WKEYS[k], CFG["w_eng"][k])
+                    if k + 3 < 8: step("ld.w%d" % (k + 3), w_load, *WKEYS[k + 3])
+            iq(("a", 1, "u"), CFG["ra_eng"][5])
+            M1("u")
+            for s in range(4):
+                chain(s, ["di"], HV)
+                roadb(s, "i")
+                if s == 1: iq(("a", 0, "i"), CFG["ra_eng"][1])
+                if s < 2:
+                    L(s, ["f0", "f1", "ncc"]); Af(s)
+            iq(("a", 1, "i"), CFG["ra_eng"][4])
+            M0(0)
+            M1("i")
+            for s in range(4):
+                if s > 0: M0(s)
+                chain(s, FCH, FULL)
+                if s + 2 < 4:
+                    L(s + 2, ["f0", "f1", "ncc"]); Af(s + 2)
+                roadb(s, "f0"); roadb(s, "f1")
+                M0f(s)
+
+        if CFG["plan"] == "slab3":
+            HV = HALves
+            step("ld.0.o.0", load_half, 0, "o", 0); step("ld.0.c.0", load_half, 0, "c", 0)
+            L(0, "g")
+            step("ld.0.o.1", load_half, 0, "o", 1); step("ld.0.c.1", load_half, 0, "c", 1)
+            L(0, "iu"); L(0, ["f0", "f1", "ncc"]); L(1, "ocg")
+            for k in range(3): step("ld.w%d" % k, w_load, *WKEYS[k])
+            for k, h in enumerate(HV):
+                step("a.to.0.%d" % k, a_tanh, 0, "o", 0.5, h)
+                step("a.tc.0.%d" % k, a_tanh, 0, "c", 1.0, h)
+                step("a.tcq.0.%d" % k, a_sq, 0, "c", "tcq", 0.5, h)
+            Aiu(0); Af(0)
+            for s in range(2):
+                Ac(s + 1)
+                chain(s, CCH, HV)
+                roadb(s, "o")
+                L(s + 2, "ocg")
+                if s == 0:
+                    L(1, "iu"); Aiu(1)
+                else:
+                    Ac(3)
+                chain(s, ICH, HV)
+                roadb(s, "i"); roadb(s, "u")
+                if s == 0:
+                    L(1, ["f0", "f1", "ncc"]); Af(1)
+                    for k in range(8):
+                        iq(("w",) + WKEYS[k], CFG["w_eng"][k])
+                        if k + 3 < 8: step("ld.w%d" % (k + 3), w_load, *WKEYS[k + 3])
+                    step("ld.nh0", nh_load, 0)
+                else:
+                    L(2, "iu"); L(3, "iu"); Aiu(2)
+                M0(s)
+                chain(s, FCH, FULL)
+                roadb(s, "f0"); roadb(s, "f1")
+                M0f(s)
+                if s == 0:
+                    for d in range(2): iq(("nh", 0, d), CFG["nh_eng"][d])
+                    step("ld.nh1", nh_load, 1)
+                if s == 1:
+                    for d in range(2): iq(("nh", 1, d), CFG["nh_eng"][2 + d])
+                    iq(("a", 0, "o"), CFG["ra_eng"][0])
+            chain(2, CCH, HV); roadb(2, "o")
+            Aiu(3)
+            chain(3, CCH, HV); roadb(3, "o")
+            iq(("a", 1, "o"), CFG["ra_eng"][3]); M1("o")
+            iq(("a", 0, "u"), CFG["ra_eng"][2])
+            L(2, ["f0", "f1", "ncc"]); Af(2)
+            chain(2, ["t1", "x", "du"], HV); roadb(2, "u")
+            chain(3, ["t1", "x", "du"], HV); roadb(3, "u")
+            iq(("a", 1, "u"), CFG["ra_eng"][5]); M1("u")
+            iq(("a", 0, "i"), CFG["ra_eng"][1])
+            L(3, ["f0", "f1", "ncc"]); Af(3)
+            chain(2, ["di"], HV); roadb(2, "i")
+            chain(3, ["di"], HV); roadb(3, "i")
+            iq(("a", 1, "i"), CFG["ra_eng"][4]); M1("i")
+            for s in (2, 3):
+                M0(s)
+                chain(s, FCH, FULL); roadb(s, "f0"); roadb(s, "f1"); M0f(s)
 
         if CFG["plan"] == "slab":
             HV = HALves

@@ -18,62 +18,10 @@ ALU = mybir.AluOpType
 P = 128
 H = 512
 GATE_ROW = {"i": 0, "o": 1, "u": 2}
-MANUAL = True
-ORDER = [
-    "ld.0.o.0", "ld.0.c.0", "ld.0.g", "ld.0.o.1", "ld.0.c.1", "ld.w0", "ld.0.i", "ld.0.u", "ld.0.f0", "a.to.0.0",
-    "ld.w1", "a.tc.0.0", "a.tcq.0.0", "v.t3.0.0", "ld.0.f1", "v.p1.0.0", "ld.w2", "a.to.0.1", "v.q.0.0",
-    "ld.0.ncc", "a.tc.0.1", "v.do.0.0", "a.tcq.0.1", "v.dcm.0.0", "ld.nh0", "ii.w0o", "v.t3.0.1", "v.p1.0.1",
-    "ld.1.o", "v.q.0.1", "v.do.0.1", "a.ti.0", "ld.1.c", "v.dcm.0.1", "tr.0.o", "iq.w0o", "a.tu.0", "ld.w3",
-    "a.tusq.0", "ld.1.g", "a.tf0.0", "v.t1.0.0", "v.t1.0.1", "a.tfsq0.0", "v.x.0.0", "ld.1.i", "v.x.0.1",
-    "a.tf1.0", "v.di.0.0", "ld.1.u", "v.di.0.1", "a.tfsq1.0", "v.du.0.0", "tr.0.i", "v.du.0.1", "ld.1.f0",
-    "ev.0.o", "v.y0.0.0", "ev.0.i", "ii.w0i", "bq.0.o", "tr.0.u", "bq.0.i", "m0o.0.0.0", "v.y1.0.0", "m0o.0.1.0",
-    "ld.1.f1", "v.df0.0.0", "ev.0.u", "iq.w0i", "ii.w0u", "ld.1.ncc", "bq.0.u", "v.df1.0.0", "tr.0.f0",
-    "m0i.0.0.0", "ld.w4", "m0i.0.1.0", "a.to.1", "iq.w0u", "ld.2.o", "ii.w0f", "tr.0.f1", "a.tc.1", "m0u.0.0.0",
-    "m0u.0.1.0", "iq.w0f", "ld.w5", "a.tcq.1", "ev.0.f0", "v.t3.1.0", "ld.2.c", "a.ti.1", "bq.0.f0", "v.t3.1.1",
-    "m0f.0.0.0", "v.p1.1.0", "ev.0.f1", "m0f.0.1.0", "ld.w6", "v.p1.1.1", "a.tu.1", "bq.0.f1", "v.q.1.0", "ld.2.g",
-    "a.tusq.1", "v.q.1.1", "v.dcm.1.0", "a.tf0.1", "ld.2.i", "v.dcm.1.1", "v.do.1.0", "a.tf1.1", "v.do.1.1",
-    "ld.2.u", "v.t1.1.0", "a.tfsq0.1", "tr.1.o", "v.t1.1.1", "v.x.1.0", "ld.2.f0", "a.tfsq1.1", "v.x.1.1",
-    "v.di.1.0", "ii.w1o", "ld.2.f1", "v.di.1.1", "v.du.1.0", "tr.1.i", "v.du.1.1", "ld.2.ncc", "v.y0.1.0",
-    "ii.w1i", "iq.w1o", "ld.3.o", "v.y1.1.0", "m0o.0.0.1", "m0o.0.1.1", "ld.w7", "v.df0.1.0", "ii.w1u", "iq.w1i",
-    "ld.3.c", "v.df1.1.0", "m0i.0.0.1", "m0i.0.1.1", "m0e.0.0.0", "ld.3.g", "ii.nh00", "m0e.0.1.0", "a.to.2",
-    "iq.w1u", "ld.3.i", "iq.nh00", "m0u.0.0.1", "a.tc.2", "ii.nh01", "m0u.0.1.1", "ld.3.u", "a.tcq.2", "iq.nh01",
-    "ev.1.o", "ld.3.f0", "v.t3.2.0", "a.ti.2", "bq.1.o", "ii.a0o", "ld.nh1", "tr.1.u", "a.tu.2", "m0o.1.0.0",
-    "m0o.1.0.1", "v.t3.2.1", "a.tusq.2", "ld.3.ncc", "m0o.1.1.0", "iq.a0o", "v.p1.2.0", "ev.1.i", "v.p1.2.1",
-    "ev.1.u", "ii.w1f", "a.tf0.2", "tr.1.f0", "a.tf1.2", "bq.1.i", "tr.1.f1", "iq.w1f", "m0i.1.0.0", "bq.1.u",
-    "a.tfsq0.2", "m0f.0.0.1", "v.q.2.0", "m0f.0.1.1", "v.q.2.1", "m0e.0.0.1", "m0u.1.0.0", "v.dcm.2.0",
-    "m0i.1.0.1", "m0e.0.1.1", "m0s.0.0", "m0u.1.0.1", "v.dcm.2.1", "m0i.1.1.0", "a.tfsq1.2", "m0u.1.1.0",
-    "v.do.2.0", "m0s.0.1", "m0o.1.1.1", "m0i.1.1.1", "v.do.2.1", "m0u.1.1.1", "ev.1.f0", "v.t1.2.0", "ld.3.f1",
-    "ev.1.f1", "bq.1.f0", "a.to.3", "v.t1.2.1", "tr.2.o", "m0f.1.0.0", "bq.1.f1", "m0f.1.1.0", "v.x.2.0",
-    "m0f.1.0.1", "m0e.1.0.0", "m0f.1.1.1", "v.x.2.1", "m0e.1.0.1", "v.di.2.0", "m0e.1.1.0", "m0s.1.0", "v.di.2.1",
-    "m0e.1.1.1", "m1a.o.0.0", "v.du.2.0", "a.tc.3", "m0s.1.1", "v.du.2.1", "tr.2.i", "v.y0.2.0", "ii.nh10",
-    "m1a.o.0.1", "v.y1.2.0", "v.df0.2.0", "ii.nh11", "iq.nh10", "v.df1.2.0", "ii.a0i", "a.tcq.3", "ev.2.o",
-    "iq.nh11", "a.ti.3", "iq.a0i", "ii.a0u", "tr.2.u", "a.tu.3", "bq.2.o", "a.tusq.3", "iq.a0u", "m0o.2.0.0",
-    "v.t3.3.0", "m0o.2.0.1", "ev.2.i", "v.t3.3.1", "m0o.2.1.0", "ev.2.u", "bq.2.i", "v.p1.3.0", "a.tf0.3",
-    "tr.2.f0", "bq.2.u", "v.p1.3.1", "tr.2.f1", "a.tf1.3", "m0i.2.0.0", "v.q.3.0", "m0u.2.0.0", "v.q.3.1",
-    "a.tfsq0.3", "m0i.2.0.1", "v.dcm.3.0", "m0u.2.0.1", "v.dcm.3.1", "m0i.2.1.0", "a.tfsq1.3", "m0u.2.1.0",
-    "v.do.3.0", "m0o.2.1.1", "m0i.2.1.1", "v.do.3.1", "ev.2.f0", "m0u.2.1.1", "v.t1.3.0", "ev.2.f1", "bq.2.f0",
-    "tr.3.o", "bq.2.f1", "m0f.2.0.0", "ev.3.o", "ii.a1o", "m0f.2.0.1", "m0e.2.0.0", "m0f.2.1.0", "m0f.2.1.1",
-    "m0e.2.0.1", "m1a.o.1.0", "bq.3.o", "m0e.2.1.0", "iq.a1o", "m0s.2.0", "m1a.o.1.1", "m0e.2.1.1", "m1a.o.2.0",
-    "v.t1.3.1", "m1b.o.0.0", "m0s.2.1", "m1b.o.0.1", "v.x.3.0", "m1e.o.0.0", "m1b.o.1.0", "m1b.o.1.1", "v.x.3.1",
-    "m1e.o.0.1", "m1b.o.2.0", "m1a.o.2.1", "v.du.3.0", "m1e.o.1.0", "m1s.o.0", "m1b.o.2.1", "m1a.o.3.0",
-    "v.du.3.1", "m1e.o.1.1", "v.di.3.0", "m1e.o.2.0", "m1b.o.3.0", "m1s.o.1", "ii.a1u", "m1e.o.2.1", "tr.3.u",
-    "m1a.o.3.1", "m1e.o.3.0", "m1s.o.2", "m1b.o.3.1", "ev.3.u", "m1a.u.0.0", "v.di.3.1", "m1a.u.0.1", "m1e.o.3.1",
-    "m1a.u.1.0", "bq.3.u", "iq.a1u", "tr.3.i", "m1s.o.3", "m1a.u.1.1", "ev.3.i", "ii.a1i", "m1a.u.2.0",
-    "m1b.u.0.0", "m1b.u.0.1", "m1e.u.0.0", "m1b.u.1.0", "m1b.u.1.1", "m1e.u.0.1", "bq.3.i", "m1b.u.2.0", "iq.a1i",
-    "m1a.u.2.1", "m1e.u.1.0", "m1s.u.0", "m1b.u.2.1", "v.y0.3.0", "m1a.u.3.0", "m1e.u.1.1", "m1b.u.3.0",
-    "m1a.u.3.1", "m1e.u.2.0", "m1s.u.1", "m1b.u.3.1", "v.y1.3.0", "m0o.3.0.0", "m1e.u.2.1", "m0i.3.0.0",
-    "m0u.3.0.0", "m1e.u.3.0", "m1s.u.2", "m0o.3.0.1", "v.df0.3.0", "m0i.3.0.1", "m1e.u.3.1", "m0u.3.0.1",
-    "m0o.3.1.0", "m1s.u.3", "m0i.3.1.0", "v.df1.3.0", "m0u.3.1.0", "tr.3.f0", "m0o.3.1.1", "ev.3.f0", "bq.3.f0",
-    "tr.3.f1", "m0i.3.1.1", "ev.3.f1", "m0u.3.1.1", "m0f.3.0.0", "bq.3.f1", "m0f.3.1.0", "m0e.3.0.0", "m0f.3.0.1",
-    "m0f.3.1.1", "m0e.3.1.0", "m0e.3.0.1", "m1a.i.0.0", "m1b.i.0.0", "m0e.3.1.1", "m0s.3.0", "m1a.i.0.1",
-    "m1e.i.0.0", "m1b.i.0.1", "m0s.3.1", "m1a.i.1.0", "m1e.i.0.1", "m1b.i.1.0", "m1a.i.1.1", "m1e.i.1.0",
-    "m1s.i.0", "m1b.i.1.1", "m1a.i.2.0", "m1e.i.1.1", "m1b.i.2.0", "m1a.i.2.1", "m1e.i.2.0", "m1s.i.1",
-    "m1b.i.2.1", "m1a.i.3.0", "m1e.i.2.1", "m1b.i.3.0", "m1a.i.3.1", "m1e.i.3.0", "m1s.i.2", "m1b.i.3.1",
-    "m1e.i.3.1", "m1s.i.3",
-]
 HOOK = None
-CFG = dict(r4=15, b4=4, tcq=2, tusq=2, dz=2, g4=3, gb=3, w=3, o0=2, o1=2, xt=2, acc=6,
-           w_eng="aaavaaav", nh_eng="vvaa", ra_eng="vvvvvv", m0_eng=["aaaa", "aaaa", "aaaa", "avav"], m1_eng=dict(o="aaaaaaaa", u="aaaaaaaa", i="avavavav"), plan="slab", w_split=4, wq="g", st_g=2)
+FAST_I = True
+BOTH = (0, 2)
+HALVES = ((0, 1), (1, 2))
 
 
 def tile_generictreelstmcell_t_v_kernel(
@@ -86,7 +34,7 @@ def tile_generictreelstmcell_t_v_kernel(
     ncc_v = neighbour_c.rearrange("(G p j) d w -> G p j d w", p=P, j=4)
     nh_v = neighbour_h.rearrange("(G p j) d w -> G p j (d w)", p=P, j=4)
     g_v = grad_out.rearrange("s (G p j) w -> G p s j w", p=P, j=4)
-    o0_v = out_0.rearrange("(G p j) d h -> G p j (d h)", p=P, j=4)
+    o0_v = out_0.rearrange("(G p j) d h -> G p j d h", p=P, j=4)
     o1_v = out_1.rearrange("d (t m) h -> t m d h", m=P)
     ui_v = U_iou.rearrange("d (g p t) h -> d g p t h", p=P, t=4)
     uf_v = U_f.rearrange("d (p t) h -> d p t h", t=4)
@@ -95,10 +43,8 @@ def tile_generictreelstmcell_t_v_kernel(
         const = ctx.enter_context(tc.tile_pool(name="const", bufs=1))
         raw = ctx.enter_context(tc.tile_pool(name="raw", bufs=2))
         keep = ctx.enter_context(tc.tile_pool(name="keep", bufs=1))
-        pst = ctx.enter_context(tc.psum_pool(name="pst", bufs=CFG["xt"]))
-        psa = ctx.enter_context(tc.psum_pool(name="psa", bufs=CFG["acc"]))
-        if MANUAL:
-            ctx.enter_context(tc.manual_schedule())
+        pst = ctx.enter_context(tc.psum_pool(name="pst", bufs=2))
+        psa = ctx.enter_context(tc.psum_pool(name="psa", bufs=6))
 
         ident = const.tile([P, P], F32, name="ident")
         make_identity(nc, ident[:])
@@ -107,88 +53,120 @@ def tile_generictreelstmcell_t_v_kernel(
         nc.scalar.activation(out=warm[:], in_=warm[:], func=ACT.Tanh)
 
         T = {}
-        prog = []
 
-        def step(label, fn, *args):
-            prog.append((label, fn, args))
+        def mark(l):
+            if HOOK is not None:
+                HOOK(l)
 
-        def rot(key, shape, dtype, tag, **kw):
-            T[key] = raw.tile(shape, dtype, name=tag, tag=tag, bufs=CFG[tag], **kw)
+        def new(key, shape, dtype, tag, bufs, align=32):
+            T[key] = raw.tile(shape, dtype, name=tag, tag=tag, bufs=bufs, align_bytes=align)
             return T[key]
 
-        def stt(out, in0, scalar, in1, op0, op1):
-            nc.vector.scalar_tensor_tensor(out=out, in0=in0, scalar=scalar, in1=in1, op0=op0, op1=op1)
-
         def where(s):
-            return s // 2, slice(2 * (s % 2), 2 * (s % 2) + 2)
+            return s // 2, 2 * (s % 2)
 
-        def load_half(s, x, k):
-            G, js = where(s)
-            if k == 0:
-                rot((s, x), [P, 2, H], F32, "r4")
-            j = 2 * (s % 2) + k
-            src = c_v[G, :, j:j + 1, :] if x == "c" else iou_v[G, :, j:j + 1, H * GATE_ROW[x]:H * GATE_ROW[x] + H]
-            nc.sync.dma_start(out=T[(s, x)][:, k:k + 1, :], in_=src)
-
-        def load(s, x):
-            G, js = where(s)
+        def load(s, x, h=BOTH):
+            mark("ld")
+            G, j0 = where(s)
+            js = slice(j0 + h[0], j0 + h[1])
+            h = slice(h[0], h[1])
+            if (s, x) not in T:
+                if x in ("g", "ncc"):
+                    new((s, x), [P, 2, 2, H], BF16, "b4", 4)
+                else:
+                    new((s, x), [P, 2, H], F32, "r4", 15)
             if x in GATE_ROW:
-                c0 = H * GATE_ROW[x]
-                nc.sync.dma_start(out=rot((s, x), [P, 2, H], F32, "r4")[:], in_=iou_v[G, :, js, c0:c0 + H])
+                nc.sync.dma_start(out=T[(s, x)][:, h, :], in_=iou_v[G, :, js, H * GATE_ROW[x]:H * GATE_ROW[x] + H])
             elif x == "c":
-                nc.sync.dma_start(out=rot((s, x), [P, 2, H], F32, "r4")[:], in_=c_v[G, :, js, :])
+                nc.sync.dma_start(out=T[(s, x)][:, h, :], in_=c_v[G, :, js, :])
             elif x == "g":
-                nc.sync.dma_start(out=rot((s, x), [P, 2, 2, H], BF16, "b4")[:], in_=g_v[G, :, :, js, :])
+                nc.sync.dma_start(out=T[(s, x)][:], in_=g_v[G, :, :, js, :])
             elif x == "ncc":
-                nc.sync.dma_start(out=rot((s, x), [P, 2, 2, H], BF16, "b4")[:], in_=ncc_v[G, :, js, :, :])
+                nc.sync.dma_start(out=T[(s, x)][:], in_=ncc_v[G, :, js, :, :])
             else:
-                nc.sync.dma_start(out=rot((s, x), [P, 2, H], F32, "r4")[:], in_=fl_v[G, :, js, int(x[1]), :])
+                nc.sync.dma_start(out=T[(s, x)][:], in_=fl_v[G, :, js, int(x[1]), :])
 
-        def act(out, in_, func, scale=1.0):
-            nc.scalar.activation(out=out, in_=in_, func=func, scale=scale)
+        def loads(s, xs):
+            for x in xs:
+                load(s, x)
 
-        def a_tanh(s, x, scale, h=slice(0, 2)):
-            act(T[(s, x)][:, h, :], T[(s, x)][:, h, :], ACT.Tanh, scale)
+        def load_w(k):
+            mark("ld")
+            d, x = WKEYS[k]
+            new(("w", d, x), [P, 4, H], BF16, "w", 3)
+            nc.sync.dma_start(out=T[("w", d, x)][:], in_=uf_v[d] if x == "f" else ui_v[d, GATE_ROW[x]])
 
-        def a_sq(s, x, new, scale, h=slice(0, 2)):
-            if new:
-                if (s, new) not in T:
-                    rot((s, new), [P, 2, H], F32, new)
-                act(T[(s, new)][:, h, :], T[(s, x)][:, h, :], ACT.Square, scale)
-            else:
-                act(T[(s, x)][:], T[(s, x)][:], ACT.Square, scale)
+        def load_nh(G):
+            mark("ld")
+            new(("nhraw", G), [P, 4, 2 * H], BF16, "nh", 1)
+            nc.sync.dma_start(out=T[("nhraw", G)][:], in_=nh_v[G])
+
+        def tanh(s, x, scale, h=BOTH):
+            mark("a")
+            h = slice(h[0], h[1])
+            nc.scalar.activation(out=T[(s, x)][:, h, :], in_=T[(s, x)][:, h, :], func=ACT.Tanh, scale=scale)
+
+        def square(s, x, to, scale, h=BOTH):
+            mark("a")
+            h = slice(h[0], h[1])
+            if (s, to) not in T:
+                new((s, to), [P, 2, H], F32, to, 2)
+            nc.scalar.activation(out=T[(s, to)][:, h, :], in_=T[(s, x)][:, h, :], func=ACT.Square, scale=scale)
+
+        def acts_c(s, hs=(BOTH,)):
+            for h in hs:
+                tanh(s, "o", 0.5, h)
+                tanh(s, "c", 1.0, h)
+                square(s, "c", "tcq", 0.5, h)
+
+        def acts_iu(s):
+            tanh(s, "i", 0.5)
+            tanh(s, "u", 1.0)
+            square(s, "u", "tusq", 1.0)
+
+        def acts_f(s):
+            tanh(s, "f0", 0.5)
+            tanh(s, "f1", 0.5)
+            square(s, "f0", "f0", 1.0)
+            square(s, "f1", "f1", 1.0)
 
         def dz(s, x):
-            G, js = where(s)
+            G, j0 = where(s)
             if ("dz", G, x) not in T:
-                tg = "dz" if CFG["plan"] in ("stage2", "stage3") else "dz" + x
-                T[("dz", G, x)] = raw.tile([P, 4, H], BF16, name=tg, tag=tg, bufs=CFG["dz"])
-            return T[("dz", G, x)][:, js, :]
+                new(("dz", G, x), [P, 4, H], BF16, "dz" + x, 2)
+            return T[("dz", G, x)][:, j0:j0 + 2, :]
 
         def dzf(s, d):
             if ("dzf", s) not in T:
-                T[("dzf", s)] = raw.tile([P, 2, 2, H], BF16, name="dzf", tag="dzf", bufs=2)
+                new(("dzf", s), [P, 2, 2, H], BF16, "dzf", 2)
             return T[("dzf", s)][:, d, :, :]
 
-        def t(s, x, h):
-            return T[(s, x)][:, h, :]
-
-        def v_op(name, s, h):
-            if name == "t3": stt(t(s, "c", h), t(s, "o", h), -1.0, t(s, "c", h), ALU.add, ALU.mult)
-            if name == "p1": stt(t(s, "o", h), t(s, "o", h), 1.0, T[(s, "g")][:, 0, h, :], ALU.add, ALU.mult)
-            if name == "q": stt(t(s, "tcq", h), t(s, "tcq", h), -0.25, t(s, "o", h), ALU.add, ALU.mult)
-            if name == "dcm": stt(t(s, "tcq", h), T[(s, "g")][:, 1, h, :], -0.5, t(s, "tcq", h), ALU.mult, ALU.add)
-            if name == "do": stt(dz(s, "o")[:, h, :], t(s, "c", h), -0.25, t(s, "o", h), ALU.mult, ALU.mult)
-            if name == "t1": stt(t(s, "u", h), t(s, "i", h), -1.0, t(s, "u", h), ALU.add, ALU.mult)
-            if name == "x": stt(t(s, "i", h), t(s, "i", h), 1.0, t(s, "tcq", h), ALU.add, ALU.mult)
-            if name == "di": stt(dz(s, "i")[:, h, :], t(s, "u", h), 0.5, t(s, "i", h), ALU.mult, ALU.mult)
-            if name == "du": stt(dz(s, "u")[:, h, :], t(s, "tusq", h), -1.0, t(s, "i", h), ALU.add, ALU.mult)
+        def v(name, s, h=BOTH):
+            mark("v")
+            h = slice(h[0], h[1])
+            def t(x):
+                return T[(s, x)][:, h, :]
+            def stt(out, in0, scalar, in1, op0, op1):
+                nc.vector.scalar_tensor_tensor(out=out, in0=in0, scalar=scalar, in1=in1, op0=op0, op1=op1)
+            if name == "t3": stt(t("c"), t("o"), -1.0, t("c"), ALU.add, ALU.mult)
+            if name == "p1": stt(t("o"), t("o"), 1.0, T[(s, "g")][:, 0, h, :], ALU.add, ALU.mult)
+            if name == "q": stt(t("tcq"), t("tcq"), -0.25, t("o"), ALU.add, ALU.mult)
+            if name == "dcm": stt(t("tcq"), T[(s, "g")][:, 1, h, :], -0.5, t("tcq"), ALU.mult, ALU.add)
+            if name == "do": stt(dz(s, "o")[:, h, :], t("c"), -0.25, t("o"), ALU.mult, ALU.mult)
+            if name == "t1": stt(t("u"), t("i"), -1.0, t("u"), ALU.add, ALU.mult)
+            if name == "x": stt(t("i"), t("i"), 1.0, t("tcq"), ALU.add, ALU.mult)
+            if name == "di": stt(dz(s, "i")[:, h, :], t("u"), 0.5, t("i"), ALU.mult, ALU.mult)
+            if name == "du": stt(dz(s, "u")[:, h, :], t("tusq"), -1.0, t("i"), ALU.add, ALU.mult)
             if name in ("y0", "y1"):
                 d = int(name[1])
-                stt(t(s, "f%d" % d, h), t(s, "f%d" % d, h), -1.0, T[(s, "ncc")][:, h, d, :], ALU.add, ALU.mult)
+                stt(t("f%d" % d), t("f%d" % d), -1.0, T[(s, "ncc")][:, h, d, :], ALU.add, ALU.mult)
             if name in ("df0", "df1"):
                 d = int(name[2])
-                stt(dzf(s, d)[:, h, :], t(s, "f%d" % d, h), 0.5, t(s, "tcq", h), ALU.mult, ALU.mult)
+                stt(dzf(s, d)[:, h, :], t("f%d" % d), 0.5, t("tcq"), ALU.mult, ALU.mult)
+
+        def pair(name, s):
+            for h in HALVES:
+                v(name, s, h)
 
         def copy_on(eng, out, in_):
             if eng == "v":
@@ -196,7 +174,8 @@ def tile_generictreelstmcell_t_v_kernel(
             else:
                 nc.scalar.copy(out=out, in_=in_)
 
-        def b_tr(s, x):
+        def tr(s, x):
+            mark("tr")
             src = dzf(s, int(x[1])) if x[0] == "f" else dz(s, x)
             xt = pst.tile([P, 2, 256], F32, name="xt", tag="xt")
             for jj in range(2):
@@ -205,481 +184,154 @@ def tile_generictreelstmcell_t_v_kernel(
                     nc.tensor.transpose(xt[:, u, P * jj:P * (jj + 1)], words[:, u:256:2], ident[:])
             T[("xt", s, x)] = xt
 
-        def b_ev(s, x, eng):
-            gb = rot(("gb", s, x), [P, 256, 4], BF16, "gb", align_bytes=64)
-            copy_on(eng, gb[:].bitcast(F32), T[("xt", s, x)][:].rearrange("q u r -> q r u"))
+        def ev(s, x):
+            mark("ev")
+            gb = new(("gb", s, x), [P, 256, 4], BF16, "gb", 3, 64)
+            nc.scalar.copy(out=gb[:].bitcast(F32), in_=T[("xt", s, x)][:].rearrange("q u r -> q r u"))
 
-        def b_q(s, x):
-            k = "f" if x[0] == "f" else "g"
-            nb = 4 if x[0] == "f" else 12
-            cb = raw.tile([P, 256], U32, name="cb" + k, tag="cb" + k, bufs=nb, align_bytes=64)
-            sb = raw.tile([P, 256], U8, name="sb" + k, tag="sb" + k, bufs=nb, align_bytes=64)
+        def bq(s, x):
+            mark("bq")
+            k, nb = ("f", 6) if x[0] == "f" else ("g", 9)
+            cb = new(("cb", s, x), [P, 256], U32, "cb" + k, nb, 64)
+            sb = new(("sb", s, x), [P, 256], U8, "sb" + k, nb, 64)
             nc.vector.quantize_mx(out=cb[:].bitcast(E5), scales=sb[:], in_=T[("gb", s, x)][:].rearrange("q r t -> q (r t)"))
-            T[("cb", s, x)] = (cb, sb)
 
-        def iq_src(key):
-            if key[0] == "w": return T[key][:]
-            if key[0] == "nh": return T[("nhraw", key[1])][:, :, H * key[2]:H * (key[2] + 1)]
-            return T[("dz", key[1], key[2])][:]
+        def ii(key, eng):
+            mark("ii")
+            if key[0] == "w":
+                src = T[key][:]
+            elif key[0] == "nh":
+                src = T[("nhraw", key[1])][:, :, H * key[2]:H * (key[2] + 1)]
+            else:
+                src = T[("dz", key[1], key[2])][:]
+            g4 = new(("g4", key), [P, H, 4], BF16, "g4", 3, 64)
+            if FAST_I:
+                copy_on(eng, g4[:].rearrange("p (w i) t -> p w t i", i=4), src.rearrange("p t (w i) -> p w t i", i=4))
+            else:
+                copy_on(eng, g4[:], src.rearrange("p t w -> p w t"))
 
-        def iq_i(key, eng):
-            g4 = rot(("g4", key), [P, H, 4], BF16, "g4", align_bytes=64)
-            copy_on(eng, g4[:], iq_src(key).rearrange("p t w -> p w t"))
-
-        def iq_q(key):
+        def iq(key):
+            mark("iq")
             nm = "%s%s%s" % key
             cd = keep.tile([P, H], U32, name="c_" + nm, align_bytes=64)
             sc = keep.tile([P, H], U8, name="s_" + nm, align_bytes=64)
-            fmt = E5 if key[0] == "a" else E4
-            nc.vector.quantize_mx(out=cd[:].bitcast(fmt), scales=sc[:], in_=T[("g4", key)][:].rearrange("p w t -> p (w t)"))
+            nc.vector.quantize_mx(out=cd[:].bitcast(E5 if key[0] == "a" else E4), scales=sc[:],
+                                  in_=T[("g4", key)][:].rearrange("p w t -> p (w t)"))
             T[("cd", key)] = (cd, sc)
 
-        def w_load(d, x):
-            q = nc.gpsimd if CFG["wq"] == "g" else nc.sync
-            q.dma_start(out=rot(("w", d, x), [P, 4, H], BF16, "w")[:], in_=uf_v[d] if x == "f" else ui_v[d, GATE_ROW[x]])
+        def mx(acc, lc, ls, cols, r, start, stop):
+            nc.tensor.matmul_mx(out=acc[:], lhsT=lc[:, cols].bitcast(E5), lhsT_scale=ls[:, cols],
+                                rhs=r[0][:].bitcast(E4), rhs_scale=r[1][:], start=start, stop=stop)
 
-        def nh_load(G):
-            T[("nhraw", G)] = raw.tile([P, 4, 2 * H], BF16, name="nh", tag="nh", bufs=1)
-            q = nc.gpsimd if CFG["wq"] == "g" else nc.sync
-            q.dma_start(out=T[("nhraw", G)][:], in_=nh_v[G])
-
-        def mx(acc, l, lcols, r, start, stop):
-            nc.tensor.matmul_mx(
-                out=acc[:], lhsT=l[0][:, lcols].bitcast(E5), lhsT_scale=l[1][:, lcols],
-                rhs=r[0][:].bitcast(E4), rhs_scale=r[1][:], start=start, stop=stop,
-            )
-
-        def m0_mm(s, jj, d, xs):
+        def m0(s, jj, d, xs):
+            mark("m0")
             if ("acc0", s, jj, d) not in T:
                 T[("acc0", s, jj, d)] = psa.tile([P, H], F32, name="acc", tag="acc")
             for x in xs:
-                mx(T[("acc0", s, jj, d)], T[("cb", s, x)], slice(P * jj, P * (jj + 1)), T[("cd", ("w", d, x[0]))], x == "o", x[0] == "f")
+                y = "f%d" % d if x == "f" else x
+                mx(T[("acc0", s, jj, d)], T[("cb", s, y)], T[("sb", s, y)], slice(P * jj, P * (jj + 1)),
+                   T[("cd", ("w", d, x))], x == "o", x == "f")
 
-        def m0_ev(s, jj, d, eng):
-            if ("o0", s, jj) not in T:
-                rot(("o0", s, jj), [P, 2 * H], F32, "r4")
-            copy_on(eng, T[("o0", s, jj)][:, H * d:H * (d + 1)], T[("acc0", s, jj, d)][:])
+        def m0_out(s, jj, engs):
+            G, j0 = where(s)
+            st = new(("o0", s, jj), [P, 2, H], F32, "r4", 15)
+            for d in range(2):
+                mark("m0e")
+                copy_on(engs[d], st[:, d, :], T[("acc0", s, jj, d)][:])
+            mark("st")
+            nc.sync.dma_start(out=o0_v[G, :, j0 + jj, :, :], in_=st[:])
 
-        def m0_st(s, jj):
-            G, js = where(s)
-            q = nc.gpsimd if s < CFG["st_g"] else nc.sync
-            q.dma_start(out=o0_v[G, :, 2 * (s % 2) + jj, :], in_=T[("o0", s, jj)][:])
-
-        def m1_mm(x, jt, d, G):
-            if G == 0:
+        def m1(x, jt, d, Gs):
+            mark("m1")
+            if 0 in Gs:
                 T[("acc1", x, jt, d)] = psa.tile([P, H], F32, name="acc", tag="acc")
-            acc = T[("acc1", x, jt, d)]
-            mx(acc, T[("cd", ("a", G, x))], slice(P * jt, P * (jt + 1)), T[("cd", ("nh", G, d))], G == 0, G == 1)
+            for G in Gs:
+                a = T[("cd", ("a", G, x))]
+                mx(T[("acc1", x, jt, d)], a[0], a[1], slice(P * jt, P * (jt + 1)), T[("cd", ("nh", G, d))], G == 0, G == 1)
 
-        def m1_ev(x, jt, d, eng):
-            if ("o1", x, jt) not in T:
-                rot(("o1", x, jt), [P, 2, H], F32, "r4")
-            copy_on(eng, T[("o1", x, jt)][:, d, :], T[("acc1", x, jt, d)][:])
+        def m1_out(x, jt, engs):
+            st = new(("o1", x, jt), [P, 2, H], F32, "r4", 15)
+            for d in range(2):
+                mark("m1e")
+                copy_on(engs[d], st[:, d, :], T[("acc1", x, jt, d)][:])
+            mark("st")
+            nc.sync.dma_start(out=o1_v[4 * GATE_ROW[x] + jt], in_=st[:])
 
-        def m1_st(x, jt):
-            nc.sync.dma_start(out=o1_v[4 * GATE_ROW[x] + jt], in_=T[("o1", x, jt)][:])
-
-        HALves = (slice(0, 1), slice(1, 2))
-        FULL = (slice(0, 2),)
-
-        def chain(s, names, halves):
-            for n in names:
-                for k, h in enumerate(halves):
-                    step("v.%s.%d.%d" % (n, s, k), v_op, n, s, h)
-
-        def roadb(s, x, eng="a"):
-            step("tr.%d.%s" % (s, x), b_tr, s, x)
-            step("ev.%d.%s" % (s, x), b_ev, s, x, eng)
-            step("bq.%d.%s" % (s, x), b_q, s, x)
-
-        def iq(key, eng):
-            nm = "%s%s%s" % key
-            step("ii." + nm, iq_i, key, eng)
-            step("iq." + nm, iq_q, key)
-
-        def M0(s, pre=True):
+        def M0(s, xs):
             for jj in range(2):
                 for d in range(2):
-                    for x in "oiu":
-                        step("m0%s.%d.%d.%d" % (x, s, jj, d), m0_mm, s, jj, d, [x])
+                    m0(s, jj, d, xs)
 
-        def M0f(s):
-            for jj in range(2):
-                for d in range(2):
-                    step("m0f.%d.%d.%d" % (s, jj, d), m0_mm, s, jj, d, ["f%d" % d])
-                    step("m0e.%d.%d.%d" % (s, jj, d), m0_ev, s, jj, d, CFG["m0_eng"][s][2 * jj + d])
-                step("m0s.%d.%d" % (s, jj), m0_st, s, jj)
-
-        def M1(x):
+        def M1(x, engs):
             for jt in range(4):
                 for d in range(2):
-                    step("m1a.%s.%d.%d" % (x, jt, d), m1_mm, x, jt, d, 0)
-                    step("m1b.%s.%d.%d" % (x, jt, d), m1_mm, x, jt, d, 1)
-                    step("m1e.%s.%d.%d" % (x, jt, d), m1_ev, x, jt, d, CFG["m1_eng"][x][2 * jt + d])
-                step("m1s.%s.%d" % (x, jt), m1_st, x, jt)
-
-        def L(s, xs):
-            for x in xs:
-                step("ld.%d.%s" % (s, x), load, s, x)
-
-        def Ac(s):
-            step("a.to.%d" % s, a_tanh, s, "o", 0.5)
-            step("a.tc.%d" % s, a_tanh, s, "c", 1.0)
-            step("a.tcq.%d" % s, a_sq, s, "c", "tcq", 0.5)
-
-        def Aiu(s):
-            step("a.ti.%d" % s, a_tanh, s, "i", 0.5)
-            step("a.tu.%d" % s, a_tanh, s, "u", 1.0)
-            step("a.tusq.%d" % s, a_sq, s, "u", "tusq", 1.0)
-
-        def Af(s):
-            for d in range(2):
-                step("a.tf%d.%d" % (d, s), a_tanh, s, "f%d" % d, 0.5)
-            for d in range(2):
-                step("a.tfsq%d.%d" % (d, s), a_sq, s, "f%d" % d, None, 1.0)
+                    m1(x, jt, d, (0, 1))
+                m1_out(x, jt, engs)
 
         WKEYS = [(d, x) for d in range(2) for x in "oiuf"]
-        CCH = ["t3", "p1", "q", "dcm", "do"]
-        ICH = ["t1", "x", "di", "du"]
-        FCH = ["y0", "y1", "df0", "df1"]
 
-        if CFG["plan"] == "stage":
-            L(0, "ocg"); L(1, "ocg"); L(2, "ocg")
-            Ac(0); Ac(1)
-            for s in range(4):
-                chain(s, CCH, HALves)
-                if s + 3 < 4: L(s + 3, "ocg")
-                if s + 2 < 4: Ac(s + 2)
-                roadb(s, "o")
-                if s == 0:
-                    L(0, "iu"); step("ld.nh0", nh_load, 0)
-                if s == 1:
-                    L(1, "iu"); Aiu(0)
-                    iq(("a", 0, "o"), CFG["ra_eng"][0])
-                if s == 2:
-                    Aiu(1)
-                    for d in range(2): iq(("nh", 0, d), CFG["nh_eng"][d])
-                    step("ld.nh1", nh_load, 1)
-                if s == 3:
-                    iq(("a", 1, "o"), CFG["ra_eng"][3])
-                    for d in range(2): iq(("nh", 1, d), CFG["nh_eng"][2 + d])
-            for s in range(4):
-                chain(s, ICH, HALves)
-                if s + 2 < 4:
-                    L(s + 2, "iu"); Aiu(s + 2)
-                if s == 0:
-                    M1("o")
-                    for k in range(3): step("ld.w%d" % k, w_load, *WKEYS[k])
-                roadb(s, "i"); roadb(s, "u")
-                if s == 1:
-                    iq(("a", 0, "i"), CFG["ra_eng"][1]); iq(("a", 0, "u"), CFG["ra_eng"][2])
-                if s >= 2:
-                    L(s - 2, ["f0", "f1", "ncc"]); Af(s - 2)
-                if CFG.get("w_early"):
-                    for k in range(2 * s, 2 * s + 2):
-                        iq(("w",) + WKEYS[k], CFG["w_eng"][k])
-                        if k + 3 < 8: step("ld.w%d" % (k + 3), w_load, *WKEYS[k + 3])
-            iq(("a", 1, "i"), CFG["ra_eng"][4]); iq(("a", 1, "u"), CFG["ra_eng"][5])
-            M1("i"); M1("u")
-            if not CFG.get("w_early"):
+        def wkey(k):
+            return ("w",) + WKEYS[k]
+
+        load(0, "o", HALVES[0]); load(0, "c", HALVES[0]); load(0, "g")
+        load(0, "o", HALVES[1]); load(0, "c", HALVES[1])
+        loads(0, ["i", "u", "f0", "f1", "ncc"]); loads(1, "ocg")
+        for k in range(3):
+            load_w(k)
+        loads(1, ["i", "u", "f0", "f1", "ncc"]); load_nh(0)
+        acts_c(0, HALVES); acts_iu(0); acts_f(0)
+
+        def road_b(s, x):
+            tr(s, x); ev(s, x); bq(s, x)
+
+        def operand(key, eng):
+            ii(key, eng); iq(key)
+
+        for s in range(4):
+            last = s == 3
+            if not last:
+                acts_c(s + 1)
+            for n in ("t3", "p1", "q", "dcm", "do"):
+                pair(n, s)
+            road_b(s, "o")
+            if not last:
+                loads(s + 1, "iu") if s > 0 else None
+                acts_iu(s + 1)
+                for n in ("t1", "x", "di", "du"):
+                    pair(n, s)
+                road_b(s, "i"); road_b(s, "u")
+                loads(s + 1, ["f0", "f1", "ncc"]) if s > 0 else None
+                acts_f(s + 1)
+            else:
+                operand(("a", 1, "o"), "v"); M1("o", "aa")
+                for n in ("t1", "x", "du"):
+                    pair(n, s)
+                road_b(s, "u")
+                operand(("a", 1, "u"), "v"); M1("u", "aa")
+                pair("di", s)
+                road_b(s, "i")
+                operand(("a", 1, "i"), "v")
+            if s == 0:
                 for k in range(8):
-                    iq(("w",) + WKEYS[k], CFG["w_eng"][k])
-                    if k + 3 < 8: step("ld.w%d" % (k + 3), w_load, *WKEYS[k + 3])
-            for s in range(4):
-                M0(s)
-                chain(s, FCH, FULL)
-                if s + 2 < 4:
-                    L(s + 2, ["f0", "f1", "ncc"]); Af(s + 2)
-                roadb(s, "f0"); roadb(s, "f1")
-                M0f(s)
-
-        if CFG["plan"] == "stage2":
-            HV = HALves
-            step("ld.0.o.0", load_half, 0, "o", 0); step("ld.0.c.0", load_half, 0, "c", 0)
-            L(0, "g")
-            step("ld.0.o.1", load_half, 0, "o", 1); step("ld.0.c.1", load_half, 0, "c", 1)
-            L(1, "ocg"); L(2, "ocg")
-            for k, h in enumerate(HV):
-                step("a.to.0.%d" % k, a_tanh, 0, "o", 0.5, h)
-                step("a.tc.0.%d" % k, a_tanh, 0, "c", 1.0, h)
-                step("a.tcq.0.%d" % k, a_sq, 0, "c", "tcq", 0.5, h)
-            Ac(1)
-            for s in range(4):
-                if s + 2 < 4: Ac(s + 2)
-                chain(s, CCH, HV)
-                if s + 3 < 4: L(s + 3, "ocg")
-                if s == 0: step("ld.nh0", nh_load, 0)
-                L(s, "iu")
-                roadb(s, "o")
-                if s == 1:
-                    iq(("a", 0, "o"), CFG["ra_eng"][0])
-                    for d in range(2): iq(("nh", 0, d), CFG["nh_eng"][d])
-                    step("ld.nh1", nh_load, 1)
-                if s >= 2: Aiu(s - 2)
-                if s == 2:
-                    for d in range(2): iq(("nh", 1, d), CFG["nh_eng"][2 + d])
-            iq(("a", 1, "o"), CFG["ra_eng"][3])
-            M1("o")
-            for k in range(3): step("ld.w%d" % k, w_load, *WKEYS[k])
-            for s in range(4):
-                if s + 2 < 4: Aiu(s + 2)
-                chain(s, ["t1", "x", "du"], HV)
-                roadb(s, "u")
-                if s == 1: iq(("a", 0, "u"), CFG["ra_eng"][2])
-            iq(("a", 1, "u"), CFG["ra_eng"][5])
-            M1("u")
-            for k in range(CFG["w_split"]):
-                iq(("w",) + WKEYS[k], CFG["w_eng"][k])
-                if k + 3 < 8: step("ld.w%d" % (k + 3), w_load, *WKEYS[k + 3])
-            for s in range(4):
-                chain(s, ["di"], HV)
-                roadb(s, "i")
-                if s == 1: iq(("a", 0, "i"), CFG["ra_eng"][1])
-                if s < 2:
-                    L(s, ["f0", "f1", "ncc"])
-            iq(("a", 1, "i"), CFG["ra_eng"][4])
-            M1("i")
-            for k in range(CFG["w_split"], 8):
-                iq(("w",) + WKEYS[k], CFG["w_eng"][k])
-                if k + 3 < 8: step("ld.w%d" % (k + 3), w_load, *WKEYS[k + 3])
-            Af(0); Af(1)
-            for s in range(4):
-                M0(s)
-                chain(s, FCH, FULL)
-                if s + 2 < 4:
-                    L(s + 2, ["f0", "f1", "ncc"]); Af(s + 2)
-                roadb(s, "f0"); roadb(s, "f1")
-                M0f(s)
-
-        if CFG["plan"] == "slab2":
-            HV = HALves
-            step("ld.0.o.0", load_half, 0, "o", 0); step("ld.0.c.0", load_half, 0, "c", 0)
-            L(0, "g")
-            step("ld.0.o.1", load_half, 0, "o", 1); step("ld.0.c.1", load_half, 0, "c", 1)
-            L(0, "iu"); L(0, ["f0", "f1", "ncc"]); L(1, "ocg")
-            for k in range(3): step("ld.w%d" % k, w_load, *WKEYS[k])
-            for k, h in enumerate(HV):
-                step("a.to.0.%d" % k, a_tanh, 0, "o", 0.5, h)
-                step("a.tc.0.%d" % k, a_tanh, 0, "c", 1.0, h)
-                step("a.tcq.0.%d" % k, a_sq, 0, "c", "tcq", 0.5, h)
-            Aiu(0); Af(0)
-            for s in range(2):
-                Ac(s + 1)
-                chain(s, CCH, HV)
-                roadb(s, "o")
-                L(s + 1, "iu"); Aiu(s + 1)
-                chain(s, ICH, HV)
-                roadb(s, "i"); roadb(s, "u")
-                L(s + 1, ["f0", "f1", "ncc"]); Af(s + 1)
-                if s == 0:
-                    for k in range(8):
-                        iq(("w",) + WKEYS[k], CFG["w_eng"][k])
-                        if k + 3 < 8: step("ld.w%d" % (k + 3), w_load, *WKEYS[k + 3])
-                    step("ld.nh0", nh_load, 0)
-                M0(s)
-                chain(s, FCH, FULL)
-                L(s + 2, "ocg")
-                roadb(s, "f0"); roadb(s, "f1")
-                M0f(s)
-                if s == 0:
-                    for d in range(2): iq(("nh", 0, d), CFG["nh_eng"][d])
-                    step("ld.nh1", nh_load, 1)
-                if s == 1:
-                    for d in range(2): iq(("nh", 1, d), CFG["nh_eng"][2 + d])
-                    iq(("a", 0, "o"), CFG["ra_eng"][0])
-            Ac(3)
-            chain(2, CCH, HV); roadb(2, "o")
-            chain(3, CCH, HV); roadb(3, "o")
-            iq(("a", 1, "o"), CFG["ra_eng"][3]); M1("o")
-            L(3, "iu"); Aiu(3)
-            iq(("a", 0, "u"), CFG["ra_eng"][2]); iq(("a", 0, "i"), CFG["ra_eng"][1])
-            chain(2, ICH, HV); roadb(2, "i"); roadb(2, "u")
-            L(3, ["f0", "f1", "ncc"]); Af(3)
-            M0(2)
-            chain(2, FCH, FULL); roadb(2, "f0"); roadb(2, "f1"); M0f(2)
-            chain(3, ["t1", "x", "du"], HV); roadb(3, "u")
-            iq(("a", 1, "u"), CFG["ra_eng"][5]); M1("u")
-            chain(3, ["di"], HV); roadb(3, "i")
-            iq(("a", 1, "i"), CFG["ra_eng"][4])
-            M0(3)
-            chain(3, FCH, FULL); roadb(3, "f0"); roadb(3, "f1"); M0f(3)
-            M1("i")
-
-        if CFG["plan"] == "stage3":
-            HV = HALves
-            step("ld.0.o.0", load_half, 0, "o", 0); step("ld.0.c.0", load_half, 0, "c", 0)
-            L(0, "g")
-            step("ld.0.o.1", load_half, 0, "o", 1); step("ld.0.c.1", load_half, 0, "c", 1)
-            L(1, "ocg"); L(2, "ocg")
-            for k, h in enumerate(HV):
-                step("a.to.0.%d" % k, a_tanh, 0, "o", 0.5, h)
-                step("a.tc.0.%d" % k, a_tanh, 0, "c", 1.0, h)
-                step("a.tcq.0.%d" % k, a_sq, 0, "c", "tcq", 0.5, h)
-            Ac(1)
-            for s in range(4):
-                if s + 2 < 4: Ac(s + 2)
-                chain(s, CCH, HV)
-                if s + 3 < 4: L(s + 3, "ocg")
-                if s == 0: step("ld.nh0", nh_load, 0)
-                L(s, "iu")
-                roadb(s, "o")
-                if s == 1:
-                    iq(("a", 0, "o"), CFG["ra_eng"][0])
-                    for d in range(2): iq(("nh", 0, d), CFG["nh_eng"][d])
-                    step("ld.nh1", nh_load, 1)
-                if s >= 1: Aiu(s - 1)
-                if s == 2:
-                    for d in range(2): iq(("nh", 1, d), CFG["nh_eng"][2 + d])
-                    for k in range(3): step("ld.w%d" % k, w_load, *WKEYS[k])
-            iq(("a", 1, "o"), CFG["ra_eng"][3])
-            M1("o")
-            Aiu(3)
-            for s in range(4):
-                chain(s, ["t1", "x", "du"], HV)
-                roadb(s, "u")
-                if s == 1: iq(("a", 0, "u"), CFG["ra_eng"][2])
-                for k in range(2 * s, 2 * s + 2):
-                    iq(("w",) + WKEYS[k], CFG["w_eng"][k])
-                    if k + 3 < 8: step("ld.w%d" % (k + 3), w_load, *WKEYS[k + 3])
-            iq(("a", 1, "u"), CFG["ra_eng"][5])
-            M1("u")
-            for s in range(4):
-                chain(s, ["di"], HV)
-                roadb(s, "i")
-                if s == 1: iq(("a", 0, "i"), CFG["ra_eng"][1])
-                if s < 2:
-                    L(s, ["f0", "f1", "ncc"]); Af(s)
-            iq(("a", 1, "i"), CFG["ra_eng"][4])
-            M0(0)
-            M1("i")
-            for s in range(4):
-                if s > 0: M0(s)
-                chain(s, FCH, FULL)
-                if s + 2 < 4:
-                    L(s + 2, ["f0", "f1", "ncc"]); Af(s + 2)
-                roadb(s, "f0"); roadb(s, "f1")
-                M0f(s)
-
-        if CFG["plan"] == "slab3":
-            HV = HALves
-            step("ld.0.o.0", load_half, 0, "o", 0); step("ld.0.c.0", load_half, 0, "c", 0)
-            L(0, "g")
-            step("ld.0.o.1", load_half, 0, "o", 1); step("ld.0.c.1", load_half, 0, "c", 1)
-            L(0, "iu"); L(0, ["f0", "f1", "ncc"]); L(1, "ocg")
-            for k in range(3): step("ld.w%d" % k, w_load, *WKEYS[k])
-            for k, h in enumerate(HV):
-                step("a.to.0.%d" % k, a_tanh, 0, "o", 0.5, h)
-                step("a.tc.0.%d" % k, a_tanh, 0, "c", 1.0, h)
-                step("a.tcq.0.%d" % k, a_sq, 0, "c", "tcq", 0.5, h)
-            Aiu(0); Af(0)
-            for s in range(2):
-                Ac(s + 1)
-                chain(s, CCH, HV)
-                roadb(s, "o")
-                L(s + 2, "ocg")
-                if s == 0:
-                    L(1, "iu"); Aiu(1)
-                else:
-                    Ac(3)
-                chain(s, ICH, HV)
-                roadb(s, "i"); roadb(s, "u")
-                if s == 0:
-                    L(1, ["f0", "f1", "ncc"]); Af(1)
-                    for k in range(8):
-                        iq(("w",) + WKEYS[k], CFG["w_eng"][k])
-                        if k + 3 < 8: step("ld.w%d" % (k + 3), w_load, *WKEYS[k + 3])
-                    step("ld.nh0", nh_load, 0)
-                else:
-                    L(2, "iu"); L(3, "iu"); Aiu(2)
-                M0(s)
-                chain(s, FCH, FULL)
-                roadb(s, "f0"); roadb(s, "f1")
-                M0f(s)
-                if s == 0:
-                    for d in range(2): iq(("nh", 0, d), CFG["nh_eng"][d])
-                    step("ld.nh1", nh_load, 1)
-                if s == 1:
-                    for d in range(2): iq(("nh", 1, d), CFG["nh_eng"][2 + d])
-                    iq(("a", 0, "o"), CFG["ra_eng"][0])
-            chain(2, CCH, HV); roadb(2, "o")
-            Aiu(3)
-            chain(3, CCH, HV); roadb(3, "o")
-            iq(("a", 1, "o"), CFG["ra_eng"][3]); M1("o")
-            iq(("a", 0, "u"), CFG["ra_eng"][2])
-            L(2, ["f0", "f1", "ncc"]); Af(2)
-            chain(2, ["t1", "x", "du"], HV); roadb(2, "u")
-            chain(3, ["t1", "x", "du"], HV); roadb(3, "u")
-            iq(("a", 1, "u"), CFG["ra_eng"][5]); M1("u")
-            iq(("a", 0, "i"), CFG["ra_eng"][1])
-            L(3, ["f0", "f1", "ncc"]); Af(3)
-            chain(2, ["di"], HV); roadb(2, "i")
-            chain(3, ["di"], HV); roadb(3, "i")
-            iq(("a", 1, "i"), CFG["ra_eng"][4]); M1("i")
-            for s in (2, 3):
-                M0(s)
-                chain(s, FCH, FULL); roadb(s, "f0"); roadb(s, "f1"); M0f(s)
-
-        if CFG["plan"] == "slab":
-            HV = HALves
-            step("ld.0.o.0", load_half, 0, "o", 0); step("ld.0.c.0", load_half, 0, "c", 0)
-            L(0, "g")
-            step("ld.0.o.1", load_half, 0, "o", 1); step("ld.0.c.1", load_half, 0, "c", 1)
-            L(0, "iu"); L(0, ["f0", "f1", "ncc"]); L(1, "ocg")
-            for k in range(3): step("ld.w%d" % k, w_load, *WKEYS[k])
-            for k, h in enumerate(HV):
-                step("a.to.0.%d" % k, a_tanh, 0, "o", 0.5, h)
-                step("a.tc.0.%d" % k, a_tanh, 0, "c", 1.0, h)
-                step("a.tcq.0.%d" % k, a_sq, 0, "c", "tcq", 0.5, h)
-            Aiu(0); Af(0)
-            for s in range(4):
-                last = s == 3
-                if s + 1 < 4:
-                    Ac(s + 1)
-                chain(s, CCH, HV)
-                roadb(s, "o")
-                if s + 1 < 4:
-                    L(s + 1, "iu"); Aiu(s + 1)
-                if last:
-                    iq(("a", 1, "o"), CFG["ra_eng"][3]); M1("o")
-                    chain(s, ["t1", "x", "du"], HV)
-                    roadb(s, "u")
-                    iq(("a", 1, "u"), CFG["ra_eng"][5]); M1("u")
-                    chain(s, ["di"], HV)
-                    roadb(s, "i")
-                    iq(("a", 1, "i"), CFG["ra_eng"][4])
-                else:
-                    chain(s, ICH, HV)
-                    roadb(s, "i"); roadb(s, "u")
-                if s + 1 < 4:
-                    L(s + 1, ["f0", "f1", "ncc"]); Af(s + 1)
-                if s == 0:
-                    for k in range(8):
-                        iq(("w",) + WKEYS[k], CFG["w_eng"][k])
-                        if k + 3 < 8: step("ld.w%d" % (k + 3), w_load, *WKEYS[k + 3])
-                    step("ld.nh0", nh_load, 0)
-                M0(s)
-                chain(s, FCH, FULL)
-                if s + 2 < 4:
-                    L(s + 2, "ocg")
-                roadb(s, "f0"); roadb(s, "f1")
-                M0f(s)
-                if last:
-                    M1("i")
-                if s == 0:
-                    for d in range(2): iq(("nh", 0, d), CFG["nh_eng"][d])
-                    step("ld.nh1", nh_load, 1)
-                if s == 1:
-                    for d in range(2): iq(("nh", 1, d), CFG["nh_eng"][2 + d])
-                    for k, x in enumerate("oiu"): iq(("a", 0, x), CFG["ra_eng"][k])
-
-        todo = prog
-        if ORDER is not None:
-            byl = {}
-            for l, fn, args in prog:
-                byl[l] = (l, fn, args)
-            todo = [byl[l] for l in ORDER]
-            assert len(todo) == len(prog)
-        for l, fn, args in todo:
-            if HOOK is not None:
-                HOOK(l)
-            fn(*args)
+                    operand(wkey(k), "v" if k % 4 == 3 else "a")
+                    if k + 3 < 8:
+                        load_w(k + 3)
+            M0(s, "oiu")
+            for n in ("y0", "y1", "df0", "df1"):
+                v(n, s)
+            if s + 2 < 4:
+                loads(s + 2, "ocg")
+            road_b(s, "f0"); road_b(s, "f1")
+            for jj in range(2):
+                for d in range(2):
+                    m0(s, jj, d, "f")
+                m0_out(s, jj, "av" if last else "aa")
+            if last:
+                M1("i", "av")
+            if s == 0:
+                operand(("nh", 0, 0), "v"); operand(("nh", 0, 1), "v")
+                load_nh(1)
+            if s == 1:
+                operand(("nh", 1, 0), "a"); operand(("nh", 1, 1), "a")
+                for x in "oiu":
+                    operand(("a", 0, x), "v")

from contextlib import ExitStack

import concourse.mybir as mybir
from concourse.masks import make_identity

FLOPS = 2 * 1024 * 1024 * (512 + 1536) + 2 * 1024 * 1536 * 1024
BYTES = 32 * 1024 * 1024

F32 = mybir.dt.float32
BF16 = mybir.dt.bfloat16
U32 = mybir.dt.uint32
U8 = mybir.dt.uint8
E4 = mybir.dt.float8_e4m3fn_x4
E5 = mybir.dt.float8_e5m2_x4
ACT = mybir.ActivationFunctionType
ALU = mybir.AluOpType

P = 128
H = 512
GATE_ROW = {"i": 0, "o": 1, "u": 2}
HOOK = None
FAST_I = True
BOTH = (0, 2)
HALVES = ((0, 1), (1, 2))


def tile_generictreelstmcell_t_v_kernel(
    tc, neighbour_h, neighbour_c, f_input, iou_input, U_f, U_iou, f_logits, iou, c, grad_out, out_0, out_1
):
    nc = tc.nc
    iou_v = iou.rearrange("(G p j) w -> G p j w", p=P, j=4)
    c_v = c.rearrange("(G p j) w -> G p j w", p=P, j=4)
    fl_v = f_logits.rearrange("(G p j) d w -> G p j d w", p=P, j=4)
    ncc_v = neighbour_c.rearrange("(G p j) d w -> G p j d w", p=P, j=4)
    nh_v = neighbour_h.rearrange("(G p j) d w -> G p j (d w)", p=P, j=4)
    g_v = grad_out.rearrange("s (G p j) w -> G p s j w", p=P, j=4)
    o0_v = out_0.rearrange("(G p j) d h -> G p j d h", p=P, j=4)
    o1_v = out_1.rearrange("d (t m) h -> t m d h", m=P)
    ui_v = U_iou.rearrange("d (g p t) h -> d g p t h", p=P, t=4)
    uf_v = U_f.rearrange("d (p t) h -> d p t h", t=4)

    with ExitStack() as ctx:
        const = ctx.enter_context(tc.tile_pool(name="const", bufs=1))
        raw = ctx.enter_context(tc.tile_pool(name="raw", bufs=2))
        keep = ctx.enter_context(tc.tile_pool(name="keep", bufs=1))
        pst = ctx.enter_context(tc.psum_pool(name="pst", bufs=2))
        psa = ctx.enter_context(tc.psum_pool(name="psa", bufs=6))

        ident = const.tile([P, P], F32, name="ident")
        make_identity(nc, ident[:])
        warm = const.tile([P, 1], F32, name="warm")
        nc.vector.memset(warm[:], 0.0)
        nc.scalar.activation(out=warm[:], in_=warm[:], func=ACT.Tanh)

        T = {}

        def mark(l):
            if HOOK is not None:
                HOOK(l)

        def new(key, shape, dtype, tag, bufs, align=32):
            T[key] = raw.tile(shape, dtype, name=tag, tag=tag, bufs=bufs, align_bytes=align)
            return T[key]

        def where(s):
            return s // 2, 2 * (s % 2)

        def load(s, x, h=BOTH):
            mark("ld")
            G, j0 = where(s)
            js = slice(j0 + h[0], j0 + h[1])
            h = slice(h[0], h[1])
            if (s, x) not in T:
                if x in ("g", "ncc"):
                    new((s, x), [P, 2, 2, H], BF16, "b4", 4)
                else:
                    new((s, x), [P, 2, H], F32, "r4", 15)
            if x in GATE_ROW:
                nc.sync.dma_start(out=T[(s, x)][:, h, :], in_=iou_v[G, :, js, H * GATE_ROW[x]:H * GATE_ROW[x] + H])
            elif x == "c":
                nc.sync.dma_start(out=T[(s, x)][:, h, :], in_=c_v[G, :, js, :])
            elif x == "g":
                nc.sync.dma_start(out=T[(s, x)][:], in_=g_v[G, :, :, js, :])
            elif x == "ncc":
                nc.sync.dma_start(out=T[(s, x)][:], in_=ncc_v[G, :, js, :, :])
            else:
                nc.sync.dma_start(out=T[(s, x)][:], in_=fl_v[G, :, js, int(x[1]), :])

        def loads(s, xs):
            for x in xs:
                load(s, x)

        def load_w(k):
            mark("ld")
            d, x = WKEYS[k]
            new(("w", d, x), [P, 4, H], BF16, "w", 3)
            nc.sync.dma_start(out=T[("w", d, x)][:], in_=uf_v[d] if x == "f" else ui_v[d, GATE_ROW[x]])

        def load_nh(G):
            mark("ld")
            new(("nhraw", G), [P, 4, 2 * H], BF16, "nh", 1)
            nc.sync.dma_start(out=T[("nhraw", G)][:], in_=nh_v[G])

        def tanh(s, x, scale, h=BOTH):
            mark("a")
            h = slice(h[0], h[1])
            nc.scalar.activation(out=T[(s, x)][:, h, :], in_=T[(s, x)][:, h, :], func=ACT.Tanh, scale=scale)

        def square(s, x, to, scale, h=BOTH):
            mark("a")
            h = slice(h[0], h[1])
            if (s, to) not in T:
                new((s, to), [P, 2, H], F32, to, 2)
            nc.scalar.activation(out=T[(s, to)][:, h, :], in_=T[(s, x)][:, h, :], func=ACT.Square, scale=scale)

        def acts_c(s, hs=(BOTH,)):
            for h in hs:
                tanh(s, "o", 0.5, h)
                tanh(s, "c", 1.0, h)
                square(s, "c", "tcq", 0.5, h)

        def acts_iu(s):
            tanh(s, "i", 0.5)
            tanh(s, "u", 1.0)
            square(s, "u", "tusq", 1.0)

        def acts_f(s):
            tanh(s, "f0", 0.5)
            tanh(s, "f1", 0.5)
            square(s, "f0", "f0", 1.0)
            square(s, "f1", "f1", 1.0)

        def dz(s, x):
            G, j0 = where(s)
            if ("dz", G, x) not in T:
                new(("dz", G, x), [P, 4, H], BF16, "dz" + x, 2)
            return T[("dz", G, x)][:, j0:j0 + 2, :]

        def dzf(s, d):
            if ("dzf", s) not in T:
                new(("dzf", s), [P, 2, 2, H], BF16, "dzf", 2)
            return T[("dzf", s)][:, d, :, :]

        def v(name, s, h=BOTH):
            mark("v")
            h = slice(h[0], h[1])
            def t(x):
                return T[(s, x)][:, h, :]
            def stt(out, in0, scalar, in1, op0, op1):
                nc.vector.scalar_tensor_tensor(out=out, in0=in0, scalar=scalar, in1=in1, op0=op0, op1=op1)
            if name == "t3": stt(t("c"), t("o"), -1.0, t("c"), ALU.add, ALU.mult)
            if name == "p1": stt(t("o"), t("o"), 1.0, T[(s, "g")][:, 0, h, :], ALU.add, ALU.mult)
            if name == "q": stt(t("tcq"), t("tcq"), -0.25, t("o"), ALU.add, ALU.mult)
            if name == "dcm": stt(t("tcq"), T[(s, "g")][:, 1, h, :], -0.5, t("tcq"), ALU.mult, ALU.add)
            if name == "do": stt(dz(s, "o")[:, h, :], t("c"), -0.25, t("o"), ALU.mult, ALU.mult)
            if name == "t1": stt(t("u"), t("i"), -1.0, t("u"), ALU.add, ALU.mult)
            if name == "x": stt(t("i"), t("i"), 1.0, t("tcq"), ALU.add, ALU.mult)
            if name == "di": stt(dz(s, "i")[:, h, :], t("u"), 0.5, t("i"), ALU.mult, ALU.mult)
            if name == "du": stt(dz(s, "u")[:, h, :], t("tusq"), -1.0, t("i"), ALU.add, ALU.mult)
            if name in ("y0", "y1"):
                d = int(name[1])
                stt(t("f%d" % d), t("f%d" % d), -1.0, T[(s, "ncc")][:, h, d, :], ALU.add, ALU.mult)
            if name in ("df0", "df1"):
                d = int(name[2])
                stt(dzf(s, d)[:, h, :], t("f%d" % d), 0.5, t("tcq"), ALU.mult, ALU.mult)

        def pair(name, s):
            for h in HALVES:
                v(name, s, h)

        def copy_on(eng, out, in_):
            if eng == "v":
                nc.vector.tensor_copy(out=out, in_=in_)
            else:
                nc.scalar.copy(out=out, in_=in_)

        def tr(s, x):
            mark("tr")
            src = dzf(s, int(x[1])) if x[0] == "f" else dz(s, x)
            xt = pst.tile([P, 2, 256], F32, name="xt", tag="xt")
            for jj in range(2):
                words = src[:, jj, :].bitcast(F32)
                for u in range(2):
                    nc.tensor.transpose(xt[:, u, P * jj:P * (jj + 1)], words[:, u:256:2], ident[:])
            T[("xt", s, x)] = xt

        def ev(s, x):
            mark("ev")
            gb = new(("gb", s, x), [P, 256, 4], BF16, "gb", 3, 64)
            nc.scalar.copy(out=gb[:].bitcast(F32), in_=T[("xt", s, x)][:].rearrange("q u r -> q r u"))

        def bq(s, x):
            mark("bq")
            k, nb = ("f", 6) if x[0] == "f" else ("g", 9)
            cb = new(("cb", s, x), [P, 256], U32, "cb" + k, nb, 64)
            sb = new(("sb", s, x), [P, 256], U8, "sb" + k, nb, 64)
            nc.vector.quantize_mx(out=cb[:].bitcast(E5), scales=sb[:], in_=T[("gb", s, x)][:].rearrange("q r t -> q (r t)"))

        def ii(key, eng):
            mark("ii")
            if key[0] == "w":
                src = T[key][:]
            elif key[0] == "nh":
                src = T[("nhraw", key[1])][:, :, H * key[2]:H * (key[2] + 1)]
            else:
                src = T[("dz", key[1], key[2])][:]
            g4 = new(("g4", key), [P, H, 4], BF16, "g4", 3, 64)
            if FAST_I:
                copy_on(eng, g4[:].rearrange("p (w i) t -> p w t i", i=4), src.rearrange("p t (w i) -> p w t i", i=4))
            else:
                copy_on(eng, g4[:], src.rearrange("p t w -> p w t"))

        def iq(key):
            mark("iq")
            nm = "%s%s%s" % key
            cd = keep.tile([P, H], U32, name="c_" + nm, align_bytes=64)
            sc = keep.tile([P, H], U8, name="s_" + nm, align_bytes=64)
            nc.vector.quantize_mx(out=cd[:].bitcast(E5 if key[0] == "a" else E4), scales=sc[:],
                                  in_=T[("g4", key)][:].rearrange("p w t -> p (w t)"))
            T[("cd", key)] = (cd, sc)

        def mx(acc, lc, ls, cols, r, start, stop):
            nc.tensor.matmul_mx(out=acc[:], lhsT=lc[:, cols].bitcast(E5), lhsT_scale=ls[:, cols],
                                rhs=r[0][:].bitcast(E4), rhs_scale=r[1][:], start=start, stop=stop)

        def m0(s, jj, d, xs):
            mark("m0")
            if ("acc0", s, jj, d) not in T:
                T[("acc0", s, jj, d)] = psa.tile([P, H], F32, name="acc", tag="acc")
            for x in xs:
                y = "f%d" % d if x == "f" else x
                mx(T[("acc0", s, jj, d)], T[("cb", s, y)], T[("sb", s, y)], slice(P * jj, P * (jj + 1)),
                   T[("cd", ("w", d, x))], x == "o", x == "f")

        def m0_out(s, jj, engs):
            G, j0 = where(s)
            st = new(("o0", s, jj), [P, 2, H], F32, "r4", 15)
            for d in range(2):
                mark("m0e")
                copy_on(engs[d], st[:, d, :], T[("acc0", s, jj, d)][:])
            mark("st")
            nc.sync.dma_start(out=o0_v[G, :, j0 + jj, :, :], in_=st[:])

        def m1(x, jt, d, Gs):
            mark("m1")
            if 0 in Gs:
                T[("acc1", x, jt, d)] = psa.tile([P, H], F32, name="acc", tag="acc")
            for G in Gs:
                a = T[("cd", ("a", G, x))]
                mx(T[("acc1", x, jt, d)], a[0], a[1], slice(P * jt, P * (jt + 1)), T[("cd", ("nh", G, d))], G == 0, G == 1)

        def m1_out(x, jt, engs):
            st = new(("o1", x, jt), [P, 2, H], F32, "r4", 15)
            for d in range(2):
                mark("m1e")
                copy_on(engs[d], st[:, d, :], T[("acc1", x, jt, d)][:])
            mark("st")
            nc.sync.dma_start(out=o1_v[4 * GATE_ROW[x] + jt], in_=st[:])

        def M0(s, xs):
            for jj in range(2):
                for d in range(2):
                    m0(s, jj, d, xs)

        def M1(x, engs):
            for jt in range(4):
                for d in range(2):
                    m1(x, jt, d, (0, 1))
                m1_out(x, jt, engs)

        WKEYS = [(d, x) for d in range(2) for x in "oiuf"]

        def wkey(k):
            return ("w",) + WKEYS[k]

        load(0, "o", HALVES[0]); load(0, "c", HALVES[0]); load(0, "g")
        load(0, "o", HALVES[1]); load(0, "c", HALVES[1])
        loads(0, ["i", "u", "f0", "f1", "ncc"]); loads(1, "ocg")
        for k in range(3):
            load_w(k)
        loads(1, ["i", "u", "f0", "f1", "ncc"]); load_nh(0)
        acts_c(0, HALVES); acts_iu(0); acts_f(0)

        def road_b(s, x):
            tr(s, x); ev(s, x); bq(s, x)

        def operand(key, eng):
            ii(key, eng); iq(key)

        for s in range(4):
            last = s == 3
            if not last:
                acts_c(s + 1)
            for n in ("t3", "p1", "q", "dcm", "do"):
                pair(n, s)
            road_b(s, "o")
            if not last:
                loads(s + 1, "iu") if s > 0 else None
                acts_iu(s + 1)
                for n in ("t1", "x", "di", "du"):
                    pair(n, s)
                road_b(s, "i"); road_b(s, "u")
                loads(s + 1, ["f0", "f1", "ncc"]) if s > 0 else None
                acts_f(s + 1)
            else:
                operand(("a", 1, "o"), "v"); M1("o", "aa")
                for n in ("t1", "x", "du"):
                    pair(n, s)
                road_b(s, "u")
                operand(("a", 1, "u"), "v"); M1("u", "aa")
                pair("di", s)
                road_b(s, "i")
                operand(("a", 1, "i"), "v")
            if s == 0:
                for k in range(8):
                    operand(wkey(k), "v" if k % 4 == 3 else "a")
                    if k + 3 < 8:
                        load_w(k + 3)
            M0(s, "oiu")
            for n in ("y0", "y1", "df0", "df1"):
                v(n, s)
            if s + 2 < 4:
                loads(s + 2, "ocg")
            road_b(s, "f0"); road_b(s, "f1")
            for jj in range(2):
                for d in range(2):
                    m0(s, jj, d, "f")
                m0_out(s, jj, "av" if last else "aa")
            if last:
                M1("i", "av")
            if s == 0:
                operand(("nh", 0, 0), "v"); operand(("nh", 0, 1), "v")
                load_nh(1)
            if s == 1:
                operand(("nh", 1, 0), "a"); operand(("nh", 1, 1), "a")
                for x in "oiu":
                    operand(("a", 0, x), "v")
